import numpy as np
import ml_dtypes


def mxq(x, axis, fmt="e4m3"):
    dtype, down = {"e4m3": (ml_dtypes.float8_e4m3fn, 7), "e5m2": (ml_dtypes.float8_e5m2, 14)}[fmt]
    v = np.moveaxis(np.asarray(x, np.float32).astype(ml_dtypes.bfloat16).astype(np.float64), axis, -1)
    blocks = v.reshape(v.shape[:-1] + (-1, 32))
    amax = np.abs(blocks).max(-1, keepdims=True)
    byte = np.maximum(np.where(amax > 0, np.frexp(amax)[1] - 1 + 127, 0) - down, 1)
    scale = np.exp2(byte - 127.0)
    codes = (blocks / scale).astype(np.float32).astype(dtype).astype(np.float64)
    return np.moveaxis((codes * scale).reshape(v.shape), -1, axis)


WIDE = False


def mx_kscale(k):
    if not WIDE:
        return np.ones(k)
    levels = np.array([10, -10, 5, -5, 0])
    a = np.random.permutation(np.resize(levels, k // 512 * 4)).reshape(k // 512, 4)
    idx = np.arange(k)
    return np.exp2(a[idx // 512, idx % 128 // 32])


BF16 = ml_dtypes.bfloat16


def bf(x):
    return np.asarray(x, np.float32).astype(BF16)


def f64(x):
    return np.asarray(x).astype(np.float64)


B, S, D, W = 2, 8192, 128, 512
NB = S // W
MASK_VALUE = -3.4028234663852886e38


def with_prev(cur, prev, op):
    return np.concatenate([cur[:, :1], op(cur[:, 1:], prev)], axis=1)


def setup_inputs():
    t = mx_kscale(W)
    top = t.max()
    f = np.concatenate([np.full(W, top), np.tile(t, NB - 1)])
    q = np.random.standard_normal((B, S, D)) * 2.0
    k = np.random.standard_normal((B, S, D))
    v = np.random.standard_normal((B, S, D)) * (top / f)[:, None]
    q[..., 0] = 8.0
    k[..., 0] += np.log(f) / (8.0 * D ** -0.5)
    return {"q": bf(q), "k": bf(k), "v": bf(v)}


def reference(q, k, v):
    scale = D ** -0.5
    qb = f64(q).reshape(B, NB, W, D)
    kt = f64(k).reshape(B, NB, W, D).transpose(0, 1, 3, 2)
    vq = mxq(f64(v).reshape(B, NB, W, D), 2, "e4m3")
    a = np.arange(W)[:, None]
    c = np.arange(W)[None, :]
    sc = np.where(c <= a, qb @ kt * scale, MASK_VALUE)
    sp = np.where(c > a, qb[:, 1:] @ kt[:, :-1] * scale, MASK_VALUE)
    m = with_prev(sc.max(-1, keepdims=True), sp.max(-1, keepdims=True), np.maximum)
    ec = np.exp(sc - m)
    ep = np.exp(sp - m[:, 1:])
    num = with_prev(mxq(ec, 3, "e4m3") @ vq, mxq(ep, 3, "e4m3") @ vq[:, :-1], np.add)
    den = with_prev(ec.sum(-1, keepdims=True), ep.sum(-1, keepdims=True), np.add)
    return (num / den).reshape(B, S, D)

@@ -1,0 +1,303 @@
+from contextlib import ExitStack
+
+import concourse.masks as masks
+import concourse.mybir as mybir
+
+F32 = mybir.dt.float32
+BF16 = mybir.dt.bfloat16
+U32 = mybir.dt.uint32
+U8 = mybir.dt.uint8
+FP8X4 = mybir.dt.float8_e4m3fn_x4
+ACTF = mybir.ActivationFunctionType
+ALU = mybir.AluOpType
+AX = mybir.AxisListType
+
+B, S, D, W = 2, 8192, 128, 512
+P = 128
+NB = S // W
+NA = W // P
+NBLK = B * NB
+NT = NBLK * NA
+SCALE = D ** -0.5
+NEG = -1.0e30
+FLOPS = 2 * (2 * NB - 1) * B * 2 * W * W * D
+
+CHUNKS = [1, 1, 2, 4, 4, 4, 4, 4, 4, 4]
+BIAS_ON_POOL = False
+DVE_EVAC = ()
+QEVAC_ON_DVE = False
+LS, LE, LV, LQ, LM = 3, 1, 1, 2, 3
+ACT_EVAC_FIRST = True
+DVE_QUANT_FIRST = True
+SM_BUFS, SD_BUFS, TP_BUFS, OB_BUFS = 2, 2, 3, 1
+LF = 1
+
+
+def tile_exactslidingwindowattention_t_kernel(tc, q, k, v, out):
+    nc = tc.nc
+    with ExitStack() as ctx:
+        ctx.enter_context(tc.manual_schedule())
+        const = ctx.enter_context(tc.tile_pool(name="const", bufs=1))
+        big = ctx.enter_context(tc.tile_pool(name="big", bufs=1))
+        raw = ctx.enter_context(tc.tile_pool(name="raw", bufs=3))
+        work = ctx.enter_context(tc.tile_pool(name="work", bufs=4))
+        small = ctx.enter_context(tc.tile_pool(name="small", bufs=4))
+        ps_sm = ctx.enter_context(tc.psum_pool(name="ps_sm", bufs=SM_BUFS))
+        ps_sd = ctx.enter_context(tc.psum_pool(name="ps_sd", bufs=SD_BUFS))
+        ps_tp = ctx.enter_context(tc.psum_pool(name="ps_tp", bufs=TP_BUFS))
+        ps_ob = ctx.enter_context(tc.psum_pool(name="ps_ob", bufs=OB_BUFS))
+
+        chunk_of = {}
+        first = 0
+        for ci, nblk in enumerate(CHUNKS):
+            for jb in range(nblk):
+                chunk_of[first + jb] = (ci, jb, nblk, first)
+            first += nblk
+        raws = {}
+
+        def load(ci):
+            nblk = CHUNKS[ci]
+            g0 = sum(CHUNKS[:ci])
+            b, r0, rows = g0 // NB, (g0 % NB) * W, nblk * W
+            kraw = raw.tile([P, 4 * NA, D], BF16, tag="kraw", name="kraw")
+            nc.sync.dma_start(out=kraw[:, 0:nblk * NA, :],
+                              in_=k[b, r0:r0 + rows, :].rearrange("(j p) d -> p j d", p=P))
+            qraw = raw.tile([P, 4 * NA, D], BF16, tag="qraw", name="qraw")
+            nc.sync.dma_start(out=qraw[:, 0:nblk * NA, :],
+                              in_=q[b, r0:r0 + rows, :].rearrange("(j p) d -> p j d", p=P))
+            vraw = raw.tile([P, 4 * 4, D], BF16, tag="vraw", name="vraw")
+            nc.sync.dma_start(out=vraw[:, 0:nblk * 4, :].rearrange("p (m e) d -> p m (e d)", e=2),
+                              in_=v[b, r0:r0 + rows, :].rearrange("(m p e) d -> p m (e d)", p=P, e=2))
+            raws[ci] = (qraw, kraw, vraw)
+
+        load(0)
+        load(1)
+        load(2)
+
+        identb = const.tile([P, P], BF16, name="identb")
+        masks.make_identity(nc, identb[:])
+        identf = const.tile([P, P], F32, name="identf")
+        masks.make_identity(nc, identf[:])
+        mdf = const.tile([P, P], F32, name="mdf")
+        nc.gpsimd.memset(mdf[:], 0.0)
+        nc.gpsimd.affine_select(out=mdf[:], in_=mdf[:], pattern=[[-1, P]], compare_op=ALU.is_ge,
+                                fill=NEG, base=0, channel_multiplier=1)
+        maf = const.tile([P, P], F32, name="maf")
+        nc.gpsimd.memset(maf[:], 0.0)
+        nc.gpsimd.affine_select(out=maf[:], in_=maf[:], pattern=[[1, P]], compare_op=ALU.is_ge,
+                                fill=NEG, base=-1, channel_multiplier=-1)
+        mask_d = const.tile([P, P], BF16, name="mask_d")
+        nc.vector.tensor_copy(out=mask_d[:], in_=mdf[:])
+        mask_a = const.tile([P, P], BF16, name="mask_a")
+        nc.vector.tensor_copy(out=mask_a[:], in_=maf[:])
+
+        qt = big.tile([P, B * S], BF16, name="qt")
+        kt = big.tile([P, B * S], BF16, name="kt")
+        vcodes = big.tile([P, NBLK, P], U32, name="vcodes", align_bytes=64)
+        vscl = big.tile([P, NBLK, P], U8, name="vscl", align_bytes=64)
+        NE = 2
+        ebufs = []
+        for s in range(NE):
+            row = []
+            for a in range(NA):
+                eb = big.tile([P, 2 * W], BF16, name="eb%d_%d" % (s, a))
+                nc.vector.memset(eb[:], 0.0)
+                row.append(eb)
+            ebufs.append(row)
+
+        st = {}
+
+        def prep_k(g):
+            ci, jb = chunk_of[g][0], chunk_of[g][1]
+            kraw = raws[ci][1]
+            tk = ps_tp.tile([P, NA, P], BF16, tag="tp", name="tk")
+            for a in range(NA):
+                nc.tensor.transpose(tk[:, a, :], kraw[:, jb * NA + a, :], identb[:])
+            st[("tk", g)] = tk
+
+        def copy_k(g):
+            tk = st.pop(("tk", g))
+            nc.vector.tensor_copy(out=kt[:, g * W:(g + 1) * W], in_=tk[:].rearrange("p a x -> p (a x)"))
+
+        def prep_q(g):
+            ci, jb = chunk_of[g][0], chunk_of[g][1]
+            qraw = raws[ci][0]
+            tq = ps_tp.tile([P, NA, P], BF16, tag="tp", name="tq")
+            for a in range(NA):
+                nc.tensor.transpose(tq[:, a, :], qraw[:, jb * NA + a, :], identb[:])
+            st[("tq", g)] = tq
+
+        def copy_q(g):
+            tq = st.pop(("tq", g))
+            if QEVAC_ON_DVE:
+                nc.vector.tensor_copy(out=qt[:, g * W:(g + 1) * W], in_=tq[:].rearrange("p a x -> p (a x)"))
+            else:
+                nc.scalar.copy(out=qt[:, g * W:(g + 1) * W], in_=tq[:].rearrange("p a x -> p (a x)"))
+
+        def prep_v(g):
+            ci, jb, nblk = chunk_of[g][0], chunk_of[g][1], chunk_of[g][2]
+            vraw = raws[ci][2]
+            vg = work.tile([P, D, 4], BF16, tag="vg", name="vg", align_bytes=64)
+            nc.vector.tensor_copy(out=vg[:].rearrange("p (c i) t -> p c t i", i=4),
+                                  in_=vraw[:, jb * 4:(jb + 1) * 4, :].rearrange("p t (c i) -> p c t i", i=4))
+            st[("vg", g)] = vg
+            if jb == nblk - 1 and ci + 3 < len(CHUNKS):
+                load(ci + 3)
+
+        def quant_v(g):
+            vg = st.pop(("vg", g))
+            nc.vector.quantize_mx(out=vcodes[:, g, :].bitcast(FP8X4), scales=vscl[:, g, :],
+                                  in_=vg[:].rearrange("p d t -> p (d t)"))
+
+        def score_diag(g):
+            sd = ps_sd.tile([P, NA, P], F32, tag="sd", name="sd")
+            for a in range(NA):
+                c0 = g * W + a * P
+                nc.tensor.matmul(sd[:, a, :], lhsT=qt[:, c0:c0 + P], rhs=kt[:, c0:c0 + P], start=True, stop=False)
+                nc.tensor.matmul(sd[:, a, :], lhsT=identb[:], rhs=mask_d[:], start=False, stop=True)
+            md = small.tile([P, NA], F32, tag="md", name="md")
+            nc.vector.tensor_reduce(out=md[:], in_=sd[:], axis=AX.X, op=ALU.max)
+            st[("sd", g)] = sd
+            st[("md", g)] = md
+            st[("mm", g)] = small.tile([P, NA], F32, tag="mm", name="mm")
+            st[("bias", g)] = small.tile([P, NA], F32, tag="bias", name="bias")
+            ssum = small.tile([P, NA, 2], F32, tag="ssum", name="ssum")
+            if g % NB == 0:
+                nc.vector.memset(ssum[:], 0.0)
+            st[("ssum", g)] = ssum
+
+        def score(i):
+            g, a = i // NA, i % NA
+            has_prev = g % NB > 0
+            c0 = i * P
+            nmain = W if has_prev else a * P
+            md, mm, bias = st[("md", g)], st[("mm", g)], st[("bias", g)]
+            eng = nc.gpsimd if BIAS_ON_POOL else nc.vector
+            if nmain > 0:
+                sm = ps_sm.tile([P, W], F32, tag="sm", name="sm")
+                st[("sm", i)] = sm
+                if has_prev:
+                    nc.tensor.matmul(sm[:], lhsT=qt[:, c0:c0 + P], rhs=kt[:, c0 - W:c0], start=True, stop=False)
+                    nc.tensor.matmul(sm[:, 0:P], lhsT=identb[:], rhs=mask_a[:], start=False, stop=True)
+                else:
+                    nc.tensor.matmul(sm[:, 0:nmain], lhsT=qt[:, c0:c0 + P], rhs=kt[:, g * W:g * W + nmain],
+                                     start=True, stop=True)
+                nc.vector.tensor_reduce(out=mm[:, a:a + 1], in_=sm[:, 0:nmain], axis=AX.X, op=ALU.max)
+                eng.tensor_scalar(out=bias[:, a:a + 1], in0=mm[:, a:a + 1], scalar1=md[:, a:a + 1],
+                                  scalar2=-SCALE, op0=ALU.max, op1=ALU.mult)
+            else:
+                eng.tensor_scalar(out=bias[:, a:a + 1], in0=md[:, a:a + 1], scalar1=-SCALE,
+                                  scalar2=0.0, op0=ALU.mult, op1=ALU.add)
+
+        def expo(i):
+            g, a = i // NA, i % NA
+            has_prev = g % NB > 0
+            nmain = W if has_prev else a * P
+            eb = ebufs[g % NE][a]
+            bias, ssum, sd = st[("bias", g)], st[("ssum", g)], st[("sd", g)]
+            if nmain > 0:
+                sm = st.pop(("sm", i))
+                e0 = a * P if has_prev else W
+                nc.scalar.activation(out=eb[:, e0:e0 + nmain], in_=sm[:, 0:nmain], func=ACTF.Exp,
+                                     bias=bias[:, a:a + 1], scale=SCALE, accum_out=ssum[:, a, 0:1])
+            nc.scalar.activation(out=eb[:, W + a * P:W + (a + 1) * P], in_=sd[:, a, :], func=ACTF.Exp,
+                                 bias=bias[:, a:a + 1], scale=SCALE, accum_out=ssum[:, a, 1:2])
+
+        def transp(i):
+            g, a = i // NA, i % NA
+            x0 = 0 if g % NB > 0 else 1
+            nx = 2 - x0
+            ew = ebufs[g % NE][a][:].bitcast(F32)
+            tp = ps_tp.tile([P, 2 * nx, P], F32, tag="tp", name="tp")
+            for gi in range(2 * nx):
+                w0 = (2 * x0 + gi) * P
+                nc.tensor.transpose(tp[:, gi, :], ew[:, w0:w0 + P], identf[:])
+            st[("tp", i)] = tp
+
+        def evac(i):
+            g = i // NA
+            nx = 2 if g % NB > 0 else 1
+            tp = st.pop(("tp", i))
+            gr = work.tile([P, nx, P, 2], F32, tag="gr", name="gr", align_bytes=64)
+            view = tp[:].rearrange("p (x u) r -> p x r u", u=2)
+            if i % 8 in DVE_EVAC:
+                nc.vector.tensor_copy(out=gr[:], in_=view)
+            else:
+                nc.scalar.copy(out=gr[:], in_=view)
+            st[("gr", i)] = gr
+
+        def quant(i):
+            g = i // NA
+            nx = 2 if g % NB > 0 else 1
+            gr = st.pop(("gr", i))
+            codes = work.tile([P, nx * P], U32, tag="codes", name="codes", align_bytes=64)
+            scl = work.tile([P, nx * P], U8, tag="scl", name="scl", align_bytes=64)
+            nc.vector.quantize_mx(out=codes[:].bitcast(FP8X4), scales=scl[:],
+                                  in_=gr[:].rearrange("p x r u -> p (x r u)").bitcast(BF16))
+            st[("codes", i)] = (codes, scl)
+
+        def pv(i):
+            g, a = i // NA, i % NA
+            x0 = 0 if g % NB > 0 else 1
+            nx = 2 - x0
+            if a == 0:
+                st[("ob", g)] = ps_ob.tile([P, NA, P], F32, tag="ob", name="ob")
+            ob = st[("ob", g)]
+            codes, scl = st.pop(("codes", i))
+            for xi in range(nx):
+                vb = g - 1 + x0 + xi
+                nc.tensor.matmul_mx(out=ob[:, a, :],
+                                    lhsT=codes[:, xi * P:(xi + 1) * P].bitcast(FP8X4),
+                                    lhsT_scale=scl[:, xi * P:(xi + 1) * P],
+                                    rhs=vcodes[:, vb, :].bitcast(FP8X4),
+                                    rhs_scale=vscl[:, vb, :],
+                                    start=(xi == 0), stop=(xi == nx - 1))
+
+        def finish(g):
+            b, n = g // NB, g % NB
+            ob, ssum = st.pop(("ob", g)), st.pop(("ssum", g))
+            den = small.tile([P, NA], F32, tag="den", name="den")
+            nc.vector.tensor_reduce(out=den[:], in_=ssum[:], axis=AX.X, op=ALU.add)
+            rden = small.tile([P, NA], F32, tag="rden", name="rden")
+            nc.vector.reciprocal(out=rden[:], in_=den[:])
+            ost = work.tile([P, NA, D], F32, tag="ost", name="ost")
+            nc.vector.tensor_tensor(out=ost[:], in0=ob[:], in1=rden[:].unsqueeze(2).to_broadcast([P, NA, D]),
+                                    op=ALU.mult)
+            nc.sync.dma_start(out=out[b, n * W:(n + 1) * W, :].rearrange("(a p) d -> p a d", p=P), in_=ost[:])
+
+        def ok(x):
+            return 0 <= x < NT
+
+        for i in range(-4 - LS, NT + LM + LF + 1):
+            js = i + LS
+            gp, r = js // NA + 1, js % NA
+            if DVE_QUANT_FIRST and ok(i - LQ):
+                quant(i - LQ)
+            if ok(js):
+                if r == 0:
+                    score_diag(js // NA)
+                score(js)
+            if not DVE_QUANT_FIRST and ok(i - LQ):
+                quant(i - LQ)
+            if ACT_EVAC_FIRST and ok(i - LV):
+                evac(i - LV)
+            if ok(i + LE):
+                expo(i + LE)
+            if ok(i):
+                transp(i)
+            if 0 <= gp < NBLK:
+                if r == 0:
+                    prep_k(gp)
+                    prep_v(gp)
+                elif r == 1:
+                    copy_k(gp)
+                    prep_q(gp)
+                    quant_v(gp)
+                elif r == 2:
+                    copy_q(gp)
+            if not ACT_EVAC_FIRST and ok(i - LV):
+                evac(i - LV)
+            if ok(i - LM):
+                pv(i - LM)
+            if ok(i - LM - LF) and (i - LM - LF) % NA == NA - 1:
+                finish((i - LM - LF) // NA)

@@ -27,10 +27,18 @@ BIAS_ON_POOL = False
 DVE_EVAC = ()
 QEVAC_ON_DVE = False
 LS, LE, LV, LQ, LM = 3, 1, 1, 2, 3
-ACT_EVAC_FIRST = True
+LX = 3
+ACT_EVAC_FIRST = False
 DVE_QUANT_FIRST = True
-SM_BUFS, SD_BUFS, TP_BUFS, OB_BUFS = 2, 2, 3, 1
-LF = 1
+SM_BUFS, SD_BUFS, TP_BUFS, OB_BUFS = 2, 2, 2, 1
+LF = 0
+LP = 0
+LC = 1
+LVP = 0
+PREP_OWN = True
+MB = 2
+PG = 3
+QK_COPY = "ad"
 
 
 def tile_exactslidingwindowattention_t_kernel(tc, q, k, v, out):
@@ -40,12 +48,13 @@ def tile_exactslidingwindowattention_t_kernel(tc, q, k, v, out):
         const = ctx.enter_context(tc.tile_pool(name="const", bufs=1))
         big = ctx.enter_context(tc.tile_pool(name="big", bufs=1))
         raw = ctx.enter_context(tc.tile_pool(name="raw", bufs=3))
-        work = ctx.enter_context(tc.tile_pool(name="work", bufs=4))
+        work = ctx.enter_context(tc.tile_pool(name="work", bufs=8))
         small = ctx.enter_context(tc.tile_pool(name="small", bufs=4))
         ps_sm = ctx.enter_context(tc.psum_pool(name="ps_sm", bufs=SM_BUFS))
         ps_sd = ctx.enter_context(tc.psum_pool(name="ps_sd", bufs=SD_BUFS))
         ps_tp = ctx.enter_context(tc.psum_pool(name="ps_tp", bufs=TP_BUFS))
         ps_ob = ctx.enter_context(tc.psum_pool(name="ps_ob", bufs=OB_BUFS))
+        ps_pr = ctx.enter_context(tc.psum_pool(name="ps_pr", bufs=1)) if PREP_OWN else ps_ob
 
         chunk_of = {}
         first = 0
@@ -107,32 +116,24 @@ def tile_exactslidingwindowattention_t_kernel(tc, q, k, v, out):
 
         st = {}
 
-        def prep_k(g):
+        def prep_qk(g):
             ci, jb = chunk_of[g][0], chunk_of[g][1]
-            kraw = raws[ci][1]
-            tk = ps_tp.tile([P, NA, P], BF16, tag="tp", name="tk")
+            qraw, kraw = raws[ci][0], raws[ci][1]
+            tqk = ps_pr.tile([P, 2, NA, P], BF16, tag="ob", name="tqk")
             for a in range(NA):
-                nc.tensor.transpose(tk[:, a, :], kraw[:, jb * NA + a, :], identb[:])
-            st[("tk", g)] = tk
-
-        def copy_k(g):
-            tk = st.pop(("tk", g))
-            nc.vector.tensor_copy(out=kt[:, g * W:(g + 1) * W], in_=tk[:].rearrange("p a x -> p (a x)"))
-
-        def prep_q(g):
-            ci, jb = chunk_of[g][0], chunk_of[g][1]
-            qraw = raws[ci][0]
-            tq = ps_tp.tile([P, NA, P], BF16, tag="tp", name="tq")
+                nc.tensor.transpose(tqk[:, 0, a, :], kraw[:, jb * NA + a, :], identb[:])
             for a in range(NA):
-                nc.tensor.transpose(tq[:, a, :], qraw[:, jb * NA + a, :], identb[:])
-            st[("tq", g)] = tq
+                nc.tensor.transpose(tqk[:, 1, a, :], qraw[:, jb * NA + a, :], identb[:])
+            st[("tqk", g)] = tqk
 
-        def copy_q(g):
-            tq = st.pop(("tq", g))
-            if QEVAC_ON_DVE:
-                nc.vector.tensor_copy(out=qt[:, g * W:(g + 1) * W], in_=tq[:].rearrange("p a x -> p (a x)"))
-            else:
-                nc.scalar.copy(out=qt[:, g * W:(g + 1) * W], in_=tq[:].rearrange("p a x -> p (a x)"))
+        def copy_qk(g):
+            tqk = st.pop(("tqk", g))
+            for s, dst in enumerate((kt, qt)):
+                view = tqk[:, s, :, :].rearrange("p a x -> p (a x)")
+                if QK_COPY[g % 2] == "d":
+                    nc.vector.tensor_copy(out=dst[:, g * W:(g + 1) * W], in_=view)
+                else:
+                    nc.scalar.copy(out=dst[:, g * W:(g + 1) * W], in_=view)
 
         def prep_v(g):
             ci, jb, nblk = chunk_of[g][0], chunk_of[g][1], chunk_of[g][2]
@@ -159,7 +160,9 @@ def tile_exactslidingwindowattention_t_kernel(tc, q, k, v, out):
             nc.vector.tensor_reduce(out=md[:], in_=sd[:], axis=AX.X, op=ALU.max)
             st[("sd", g)] = sd
             st[("md", g)] = md
-            st[("mm", g)] = small.tile([P, NA], F32, tag="mm", name="mm")
+            bd = small.tile([P, NA], F32, tag="bd", name="bd")
+            nc.vector.tensor_scalar(out=bd[:], in0=md[:], scalar1=-SCALE, scalar2=None, op0=ALU.mult)
+            st[("bd", g)] = bd
             st[("bias", g)] = small.tile([P, NA], F32, tag="bias", name="bias")
             ssum = small.tile([P, NA, 2], F32, tag="ssum", name="ssum")
             if g % NB == 0:
@@ -171,35 +174,41 @@ def tile_exactslidingwindowattention_t_kernel(tc, q, k, v, out):
             has_prev = g % NB > 0
             c0 = i * P
             nmain = W if has_prev else a * P
-            md, mm, bias = st[("md", g)], st[("mm", g)], st[("bias", g)]
-            eng = nc.gpsimd if BIAS_ON_POOL else nc.vector
-            if nmain > 0:
-                sm = ps_sm.tile([P, W], F32, tag="sm", name="sm")
-                st[("sm", i)] = sm
-                if has_prev:
-                    nc.tensor.matmul(sm[:], lhsT=qt[:, c0:c0 + P], rhs=kt[:, c0 - W:c0], start=True, stop=False)
-                    nc.tensor.matmul(sm[:, 0:P], lhsT=identb[:], rhs=mask_a[:], start=False, stop=True)
-                else:
-                    nc.tensor.matmul(sm[:, 0:nmain], lhsT=qt[:, c0:c0 + P], rhs=kt[:, g * W:g * W + nmain],
-                                     start=True, stop=True)
-                nc.vector.tensor_reduce(out=mm[:, a:a + 1], in_=sm[:, 0:nmain], axis=AX.X, op=ALU.max)
-                eng.tensor_scalar(out=bias[:, a:a + 1], in0=mm[:, a:a + 1], scalar1=md[:, a:a + 1],
-                                  scalar2=-SCALE, op0=ALU.max, op1=ALU.mult)
+            if nmain == 0:
+                return
+            sm = ps_sm.tile([P, W], F32, tag="sm", name="sm")
+            st[("sm", i)] = sm
+            if has_prev:
+                nc.tensor.matmul(sm[:], lhsT=qt[:, c0:c0 + P], rhs=kt[:, c0 - W:c0], start=True, stop=False)
+                nc.tensor.matmul(sm[:, 0:P], lhsT=identb[:], rhs=mask_a[:], start=False, stop=True)
             else:
-                eng.tensor_scalar(out=bias[:, a:a + 1], in0=md[:, a:a + 1], scalar1=-SCALE,
-                                  scalar2=0.0, op0=ALU.mult, op1=ALU.add)
+                nc.tensor.matmul(sm[:, 0:nmain], lhsT=qt[:, c0:c0 + P], rhs=kt[:, g * W:g * W + nmain],
+                                 start=True, stop=True)
+
+        def rowmax(i):
+            g, a = i // NA, i % NA
+            nmain = W if g % NB > 0 else a * P
+            if nmain == 0:
+                return
+            sm = st.pop(("sm", i))
+            ss = work.tile([P, W], F32, tag="ss", name="ss")
+            st[("ss", i)] = ss
+            nc.vector.tensor_scalar(out=ss[:, 0:nmain], in0=sm[:, 0:nmain], scalar1=-SCALE,
+                                    scalar2=st[("bd", g)][:, a:a + 1], op0=ALU.mult, op1=ALU.min,
+                                    accum_out=st[("bias", g)][:, a:a + 1])
 
         def expo(i):
             g, a = i // NA, i % NA
             has_prev = g % NB > 0
             nmain = W if has_prev else a * P
             eb = ebufs[g % NE][a]
-            bias, ssum, sd = st[("bias", g)], st[("ssum", g)], st[("sd", g)]
+            ssum, sd = st[("ssum", g)], st[("sd", g)]
+            bias = st[("bias", g)] if nmain > 0 else st[("bd", g)]
             if nmain > 0:
-                sm = st.pop(("sm", i))
+                ss = st.pop(("ss", i))
                 e0 = a * P if has_prev else W
-                nc.scalar.activation(out=eb[:, e0:e0 + nmain], in_=sm[:, 0:nmain], func=ACTF.Exp,
-                                     bias=bias[:, a:a + 1], scale=SCALE, accum_out=ssum[:, a, 0:1])
+                nc.scalar.activation(out=eb[:, e0:e0 + nmain], in_=ss[:, 0:nmain], func=ACTF.Exp,
+                                     bias=bias[:, a:a + 1], scale=-1.0, accum_out=ssum[:, a, 0:1])
             nc.scalar.activation(out=eb[:, W + a * P:W + (a + 1) * P], in_=sd[:, a, :], func=ACTF.Exp,
                                  bias=bias[:, a:a + 1], scale=SCALE, accum_out=ssum[:, a, 1:2])
 
@@ -268,15 +277,19 @@ def tile_exactslidingwindowattention_t_kernel(tc, q, k, v, out):
         def ok(x):
             return 0 <= x < NT
 
-        for i in range(-4 - LS, NT + LM + LF + 1):
+        def okb(x):
+            return 0 <= x < NBLK
+
+        for i in range(-4 * PG + LM + LP - 1, NT + LM + LF + 1):
             js = i + LS
-            gp, r = js // NA + 1, js % NA
             if DVE_QUANT_FIRST and ok(i - LQ):
                 quant(i - LQ)
             if ok(js):
-                if r == 0:
+                if js % NA == 0:
                     score_diag(js // NA)
                 score(js)
+            if ok(i + LX):
+                rowmax(i + LX)
             if not DVE_QUANT_FIRST and ok(i - LQ):
                 quant(i - LQ)
             if ACT_EVAC_FIRST and ok(i - LV):
@@ -285,19 +298,24 @@ def tile_exactslidingwindowattention_t_kernel(tc, q, k, v, out):
                 expo(i + LE)
             if ok(i):
                 transp(i)
-            if 0 <= gp < NBLK:
-                if r == 0:
-                    prep_k(gp)
-                    prep_v(gp)
-                elif r == 1:
-                    copy_k(gp)
-                    prep_q(gp)
-                    quant_v(gp)
-                elif r == 2:
-                    copy_q(gp)
             if not ACT_EVAC_FIRST and ok(i - LV):
                 evac(i - LV)
-            if ok(i - LM):
-                pv(i - LM)
-            if ok(i - LM - LF) and (i - LM - LF) % NA == NA - 1:
-                finish((i - LM - LF) // NA)
+            z = i - LM
+            if z % MB == MB - 1 and ok(z):
+                for a in range(MB):
+                    pv(z - MB + 1 + a)
+            z = i - LM - LF
+            if z % NA == NA - 1 and okb(z // NA):
+                finish(z // NA)
+            z = i - LM - LP
+            if z % NA == NA - 1 and okb(z // NA + PG):
+                prep_qk(z // NA + PG)
+            z = i - LM - LP - LC
+            if z % NA == NA - 1 and okb(z // NA + PG):
+                copy_qk(z // NA + PG)
+            z = i - LM - LP - LVP
+            if z % NA == NA - 1 and okb(z // NA + PG):
+                prep_v(z // NA + PG)
+            z = i - LM - LP - LVP - 1
+            if z % NA == NA - 1 and okb(z // NA + PG):
+                quant_v(z // NA + PG)

@@ -44,7 +44,6 @@ QK_COPY = "ad"
 def tile_exactslidingwindowattention_t_kernel(tc, q, k, v, out):
     nc = tc.nc
     with ExitStack() as ctx:
-        ctx.enter_context(tc.manual_schedule())
         const = ctx.enter_context(tc.tile_pool(name="const", bufs=1))
         big = ctx.enter_context(tc.tile_pool(name="big", bufs=1))
         raw = ctx.enter_context(tc.tile_pool(name="raw", bufs=3))

@@ -6,6 +6,7 @@ import concourse.mybir as mybir
 F32 = mybir.dt.float32
 BF16 = mybir.dt.bfloat16
 U32 = mybir.dt.uint32
+I32 = mybir.dt.int32
 U8 = mybir.dt.uint8
 FP8X4 = mybir.dt.float8_e4m3fn_x4
 ACTF = mybir.ActivationFunctionType
@@ -18,27 +19,20 @@ NB = S // W
 NA = W // P
 NBLK = B * NB
 NT = NBLK * NA
+NY = NA + 1
+RW = NY * P
 SCALE = D ** -0.5
 NEG = -1.0e30
 FLOPS = 2 * (2 * NB - 1) * B * 2 * W * W * D
 
 CHUNKS = [1, 1, 2, 4, 4, 4, 4, 4, 4, 4]
-BIAS_ON_POOL = False
-DVE_EVAC = ()
-QEVAC_ON_DVE = False
 LS, LE, LV, LQ, LM = 3, 1, 1, 2, 3
-LX = 3
-ACT_EVAC_FIRST = False
-DVE_QUANT_FIRST = True
 SM_BUFS, SD_BUFS, TP_BUFS, OB_BUFS = 2, 2, 2, 1
-LF = 0
-LP = 0
-LC = 1
-LVP = 0
-PREP_OWN = True
-MB = 2
 PG = 3
+NV = 6
+NE = 2
 QK_COPY = "ad"
+GROUPS = {1: (0, 1), 2: (2,), 3: (3, 4)}
 
 
 def tile_exactslidingwindowattention_t_kernel(tc, q, k, v, out):
@@ -47,13 +41,13 @@ def tile_exactslidingwindowattention_t_kernel(tc, q, k, v, out):
         const = ctx.enter_context(tc.tile_pool(name="const", bufs=1))
         big = ctx.enter_context(tc.tile_pool(name="big", bufs=1))
         raw = ctx.enter_context(tc.tile_pool(name="raw", bufs=3))
-        work = ctx.enter_context(tc.tile_pool(name="work", bufs=8))
+        work = ctx.enter_context(tc.tile_pool(name="work", bufs=6))
         small = ctx.enter_context(tc.tile_pool(name="small", bufs=4))
         ps_sm = ctx.enter_context(tc.psum_pool(name="ps_sm", bufs=SM_BUFS))
         ps_sd = ctx.enter_context(tc.psum_pool(name="ps_sd", bufs=SD_BUFS))
         ps_tp = ctx.enter_context(tc.psum_pool(name="ps_tp", bufs=TP_BUFS))
         ps_ob = ctx.enter_context(tc.psum_pool(name="ps_ob", bufs=OB_BUFS))
-        ps_pr = ctx.enter_context(tc.psum_pool(name="ps_pr", bufs=1)) if PREP_OWN else ps_ob
+        ps_pr = ctx.enter_context(tc.psum_pool(name="ps_pr", bufs=1))
 
         chunk_of = {}
         first = 0
@@ -74,8 +68,8 @@ def tile_exactslidingwindowattention_t_kernel(tc, q, k, v, out):
             nc.sync.dma_start(out=qraw[:, 0:nblk * NA, :],
                               in_=q[b, r0:r0 + rows, :].rearrange("(j p) d -> p j d", p=P))
             vraw = raw.tile([P, 4 * 4, D], BF16, tag="vraw", name="vraw")
-            nc.sync.dma_start(out=vraw[:, 0:nblk * 4, :].rearrange("p (m e) d -> p m (e d)", e=2),
-                              in_=v[b, r0:r0 + rows, :].rearrange("(m p e) d -> p m (e d)", p=P, e=2))
+            nc.sync.dma_start(out=vraw[:, 0:nblk * 4, :].rearrange("p (m t) d -> p m (t d)", t=4),
+                              in_=v[b, r0:r0 + rows, :].rearrange("(m p t) d -> p m (t d)", p=P, t=4))
             raws[ci] = (qraw, kraw, vraw)
 
         load(0)
@@ -103,22 +97,24 @@ def tile_exactslidingwindowattention_t_kernel(tc, q, k, v, out):
         kt = big.tile([P, B * S], BF16, name="kt")
         vcodes = big.tile([P, NBLK, P], U32, name="vcodes", align_bytes=64)
         vscl = big.tile([P, NBLK, P], U8, name="vscl", align_bytes=64)
-        NE = 2
-        ebufs = []
+        vzs = []
+        for s in range(NV):
+            vz = big.tile([P, 2 * (NA - 1), P], U32, name="vz%d" % s, align_bytes=64)
+            nc.gpsimd.memset(vz[:], 0)
+            vzs.append(vz)
+        ebs = []
         for s in range(NE):
-            row = []
-            for a in range(NA):
-                eb = big.tile([P, 2 * W], BF16, name="eb%d_%d" % (s, a))
+            eb = big.tile([P, 2, 2 * RW], BF16, name="eb%d" % s)
+            if s == 0:
                 nc.vector.memset(eb[:], 0.0)
-                row.append(eb)
-            ebufs.append(row)
+            ebs.append(eb)
 
         st = {}
 
         def prep_qk(g):
             ci, jb = chunk_of[g][0], chunk_of[g][1]
             qraw, kraw = raws[ci][0], raws[ci][1]
-            tqk = ps_pr.tile([P, 2, NA, P], BF16, tag="ob", name="tqk")
+            tqk = ps_pr.tile([P, 2, NA, P], BF16, tag="pr", name="tqk")
             for a in range(NA):
                 nc.tensor.transpose(tqk[:, 0, a, :], kraw[:, jb * NA + a, :], identb[:])
             for a in range(NA):
@@ -148,6 +144,11 @@ def tile_exactslidingwindowattention_t_kernel(tc, q, k, v, out):
             vg = st.pop(("vg", g))
             nc.vector.quantize_mx(out=vcodes[:, g, :].bitcast(FP8X4), scales=vscl[:, g, :],
                                   in_=vg[:].rearrange("p d t -> p (d t)"))
+            vz = vzs[g % NV]
+            for i in range(NA):
+                r = slice(i * 32, (i + 1) * 32)
+                nc.sync.dma_start(out=vz[r, i:i + NA - 1, :].bitcast(I32),
+                                  in_=vcodes[r, g, :].bitcast(I32).unsqueeze(1).to_broadcast([32, NA - 1, P]))
 
         def score_diag(g):
             sd = ps_sd.tile([P, NA, P], F32, tag="sd", name="sd")
@@ -158,7 +159,6 @@ def tile_exactslidingwindowattention_t_kernel(tc, q, k, v, out):
             md = small.tile([P, NA], F32, tag="md", name="md")
             nc.vector.tensor_reduce(out=md[:], in_=sd[:], axis=AX.X, op=ALU.max)
             st[("sd", g)] = sd
-            st[("md", g)] = md
             bd = small.tile([P, NA], F32, tag="bd", name="bd")
             nc.vector.tensor_scalar(out=bd[:], in0=md[:], scalar1=-SCALE, scalar2=None, op0=ALU.mult)
             st[("bd", g)] = bd
@@ -168,16 +168,19 @@ def tile_exactslidingwindowattention_t_kernel(tc, q, k, v, out):
                 nc.vector.memset(ssum[:], 0.0)
             st[("ssum", g)] = ssum
 
-        def score(i):
+        def n_main(i):
             g, a = i // NA, i % NA
-            has_prev = g % NB > 0
+            return W if g % NB > 0 else a * P
+
+        def score(i):
+            g = i // NA
             c0 = i * P
-            nmain = W if has_prev else a * P
+            nmain = n_main(i)
             if nmain == 0:
                 return
             sm = ps_sm.tile([P, W], F32, tag="sm", name="sm")
             st[("sm", i)] = sm
-            if has_prev:
+            if g % NB > 0:
                 nc.tensor.matmul(sm[:], lhsT=qt[:, c0:c0 + P], rhs=kt[:, c0 - W:c0], start=True, stop=False)
                 nc.tensor.matmul(sm[:, 0:P], lhsT=identb[:], rhs=mask_a[:], start=False, stop=True)
             else:
@@ -186,7 +189,7 @@ def tile_exactslidingwindowattention_t_kernel(tc, q, k, v, out):
 
         def rowmax(i):
             g, a = i // NA, i % NA
-            nmain = W if g % NB > 0 else a * P
+            nmain = n_main(i)
             if nmain == 0:
                 return
             sm = st.pop(("sm", i))
@@ -198,68 +201,74 @@ def tile_exactslidingwindowattention_t_kernel(tc, q, k, v, out):
 
         def expo(i):
             g, a = i // NA, i % NA
-            has_prev = g % NB > 0
-            nmain = W if has_prev else a * P
-            eb = ebufs[g % NE][a]
+            nmain = n_main(i)
+            eb = ebs[g % NE]
             ssum, sd = st[("ssum", g)], st[("sd", g)]
             bias = st[("bias", g)] if nmain > 0 else st[("bd", g)]
+            end = (a + 1) * 2 * (P + 32)
+            dg = end - P // 2
             if nmain > 0:
                 ss = st.pop(("ss", i))
-                e0 = a * P if has_prev else W
-                nc.scalar.activation(out=eb[:, e0:e0 + nmain], in_=ss[:, 0:nmain], func=ACTF.Exp,
-                                     bias=bias[:, a:a + 1], scale=-1.0, accum_out=ssum[:, a, 0:1])
-            nc.scalar.activation(out=eb[:, W + a * P:W + (a + 1) * P], in_=sd[:, a, :], func=ACTF.Exp,
-                                 bias=bias[:, a:a + 1], scale=SCALE, accum_out=ssum[:, a, 1:2])
+                nc.scalar.activation(out=eb[:, :, dg - nmain // 2:dg].rearrange("p u (x e) -> p u x e", e=2),
+                                     in_=ss[:, 0:nmain].rearrange("p (x u e) -> p u x e", u=2, e=2),
+                                     func=ACTF.Exp, bias=bias[:, a:a + 1], scale=-1.0, accum_out=ssum[:, a, 0:1])
+            nc.scalar.activation(out=eb[:, :, dg:end].rearrange("p u (x e) -> p u x e", e=2),
+                                 in_=sd[:, a, :].rearrange("p (x u e) -> p u x e", u=2, e=2),
+                                 func=ACTF.Exp, bias=bias[:, a:a + 1], scale=SCALE, accum_out=ssum[:, a, 1:2])
+
+        def groups(i):
+            g, a = i // NA, i % NA
+            ys = GROUPS.get(a, ())
+            return [y for y in ys if y > 0 or g % NB > 0]
 
         def transp(i):
-            g, a = i // NA, i % NA
-            x0 = 0 if g % NB > 0 else 1
-            nx = 2 - x0
-            ew = ebufs[g % NE][a][:].bitcast(F32)
-            tp = ps_tp.tile([P, 2 * nx, P], F32, tag="tp", name="tp")
-            for gi in range(2 * nx):
-                w0 = (2 * x0 + gi) * P
-                nc.tensor.transpose(tp[:, gi, :], ew[:, w0:w0 + P], identf[:])
+            ys = groups(i)
+            if not ys:
+                return
+            ew = ebs[(i // NA) % NE][:].bitcast(F32)
+            tp = ps_tp.tile([P, len(ys), 2, P], F32, tag="tp", name="tp")
+            for s, y in enumerate(ys):
+                for u in range(2):
+                    nc.tensor.transpose(tp[:, s, u, :], ew[:, u, y * P:(y + 1) * P], identf[:])
             st[("tp", i)] = tp
 
         def evac(i):
-            g = i // NA
-            nx = 2 if g % NB > 0 else 1
+            n = len(groups(i))
+            if n == 0:
+                return
             tp = st.pop(("tp", i))
-            gr = work.tile([P, nx, P, 2], F32, tag="gr", name="gr", align_bytes=64)
-            view = tp[:].rearrange("p (x u) r -> p x r u", u=2)
-            if i % 8 in DVE_EVAC:
-                nc.vector.tensor_copy(out=gr[:], in_=view)
-            else:
-                nc.scalar.copy(out=gr[:], in_=view)
+            gr = work.tile([P, n, P, 2], F32, tag="gr", name="gr", align_bytes=64)
+            nc.scalar.copy(out=gr[:], in_=tp[:].rearrange("p s u r -> p s r u"))
             st[("gr", i)] = gr
 
         def quant(i):
             g = i // NA
-            nx = 2 if g % NB > 0 else 1
+            ys = groups(i)
+            if not ys:
+                return
+            n = len(ys)
             gr = st.pop(("gr", i))
-            codes = work.tile([P, nx * P], U32, tag="codes", name="codes", align_bytes=64)
-            scl = work.tile([P, nx * P], U8, tag="scl", name="scl", align_bytes=64)
+            codes = work.tile([P, n * P], U32, tag="codes", name="codes", align_bytes=64)
+            scl = work.tile([P, n * P], U8, tag="scl", name="scl", align_bytes=64)
             nc.vector.quantize_mx(out=codes[:].bitcast(FP8X4), scales=scl[:],
-                                  in_=gr[:].rearrange("p x r u -> p (x r u)").bitcast(BF16))
-            st[("codes", i)] = (codes, scl)
+                                  in_=gr[:].rearrange("p s r u -> p (s r u)").bitcast(BF16))
+            for s, y in enumerate(ys):
+                st[("codes", g, y)] = (codes[:, s * P:(s + 1) * P], scl[:, s * P:(s + 1) * P])
 
         def pv(i):
             g, a = i // NA, i % NA
-            x0 = 0 if g % NB > 0 else 1
-            nx = 2 - x0
             if a == 0:
                 st[("ob", g)] = ps_ob.tile([P, NA, P], F32, tag="ob", name="ob")
             ob = st[("ob", g)]
-            codes, scl = st.pop(("codes", i))
-            for xi in range(nx):
-                vb = g - 1 + x0 + xi
-                nc.tensor.matmul_mx(out=ob[:, a, :],
-                                    lhsT=codes[:, xi * P:(xi + 1) * P].bitcast(FP8X4),
-                                    lhsT_scale=scl[:, xi * P:(xi + 1) * P],
-                                    rhs=vcodes[:, vb, :].bitcast(FP8X4),
-                                    rhs_scale=vscl[:, vb, :],
-                                    start=(xi == 0), stop=(xi == nx - 1))
+            terms = []
+            if g % NB > 0:
+                terms.append((a, g - 1, vcodes[:, g - 1, :] if a == 0 else vzs[(g - 1) % NV][:, 2 + a, :]))
+            terms.append((a + 1, g, vcodes[:, g, :] if a == NA - 1 else vzs[g % NV][:, a, :]))
+            for x, (y, vb, vc) in enumerate(terms):
+                codes, scl = st[("codes", g, y)]
+                nc.tensor.matmul_mx(out=ob[:, a, :], lhsT=codes.bitcast(FP8X4), lhsT_scale=scl,
+                                    rhs=vc.bitcast(FP8X4), rhs_scale=vscl[:, vb, :],
+                                    start=(x == 0), stop=(x == len(terms) - 1))
 
         def finish(g):
             b, n = g // NB, g % NB
@@ -279,42 +288,31 @@ def tile_exactslidingwindowattention_t_kernel(tc, q, k, v, out):
         def okb(x):
             return 0 <= x < NBLK
 
-        for i in range(-4 * PG + LM + LP - 1, NT + LM + LF + 1):
+        for i in range(-4 * PG + LM - 1, NT + LM + 1):
             js = i + LS
-            if DVE_QUANT_FIRST and ok(i - LQ):
+            if ok(i - LQ):
                 quant(i - LQ)
             if ok(js):
                 if js % NA == 0:
                     score_diag(js // NA)
                 score(js)
-            if ok(i + LX):
-                rowmax(i + LX)
-            if not DVE_QUANT_FIRST and ok(i - LQ):
-                quant(i - LQ)
-            if ACT_EVAC_FIRST and ok(i - LV):
-                evac(i - LV)
+                rowmax(js)
             if ok(i + LE):
                 expo(i + LE)
             if ok(i):
                 transp(i)
-            if not ACT_EVAC_FIRST and ok(i - LV):
+            if ok(i - LV):
                 evac(i - LV)
             z = i - LM
-            if z % MB == MB - 1 and ok(z):
-                for a in range(MB):
-                    pv(z - MB + 1 + a)
-            z = i - LM - LF
+            if z % NA >= 2 and ok(z):
+                for a in ((0, 1) if z % NA == 2 else (2, 3)):
+                    pv(z // NA * NA + a)
             if z % NA == NA - 1 and okb(z // NA):
                 finish(z // NA)
-            z = i - LM - LP
             if z % NA == NA - 1 and okb(z // NA + PG):
                 prep_qk(z // NA + PG)
-            z = i - LM - LP - LC
+                prep_v(z // NA + PG)
+            z = i - LM - 1
             if z % NA == NA - 1 and okb(z // NA + PG):
                 copy_qk(z // NA + PG)
-            z = i - LM - LP - LVP
-            if z % NA == NA - 1 and okb(z // NA + PG):
-                prep_v(z // NA + PG)
-            z = i - LM - LP - LVP - 1
-            if z % NA == NA - 1 and okb(z // NA + PG):
                 quant_v(z // NA + PG)

@@ -26,9 +26,7 @@ NEG = -1.0e30
 FLOPS = 2 * (2 * NB - 1) * B * 2 * W * W * D
 
 CHUNKS = [1, 1, 2, 4, 4, 4, 4, 4, 4, 4]
-LS, LE, LV, LQ, LM = 3, 1, 1, 2, 3
 SM_BUFS, SD_BUFS, TP_BUFS, OB_BUFS = 2, 2, 2, 1
-PG = 3
 NV = 6
 NE = 2
 QK_COPY = "ad"
@@ -121,14 +119,13 @@ def tile_exactslidingwindowattention_t_kernel(tc, q, k, v, out):
                 nc.tensor.transpose(tqk[:, 1, a, :], qraw[:, jb * NA + a, :], identb[:])
             st[("tqk", g)] = tqk
 
-        def copy_qk(g):
-            tqk = st.pop(("tqk", g))
-            for s, dst in enumerate((kt, qt)):
-                view = tqk[:, s, :, :].rearrange("p a x -> p (a x)")
-                if QK_COPY[g % 2] == "d":
-                    nc.vector.tensor_copy(out=dst[:, g * W:(g + 1) * W], in_=view)
-                else:
-                    nc.scalar.copy(out=dst[:, g * W:(g + 1) * W], in_=view)
+        def copy_qk(g, s):
+            dst = (kt, qt)[s]
+            view = st[("tqk", g)][:, s, :, :].rearrange("p a x -> p (a x)")
+            if QK_COPY[g % 2] == "d":
+                nc.vector.tensor_copy(out=dst[:, g * W:(g + 1) * W], in_=view)
+            else:
+                nc.scalar.copy(out=dst[:, g * W:(g + 1) * W], in_=view)
 
         def prep_v(g):
             ci, jb, nblk = chunk_of[g][0], chunk_of[g][1], chunk_of[g][2]
@@ -156,11 +153,16 @@ def tile_exactslidingwindowattention_t_kernel(tc, q, k, v, out):
                 c0 = g * W + a * P
                 nc.tensor.matmul(sd[:, a, :], lhsT=qt[:, c0:c0 + P], rhs=kt[:, c0:c0 + P], start=True, stop=False)
                 nc.tensor.matmul(sd[:, a, :], lhsT=identb[:], rhs=mask_d[:], start=False, stop=True)
-            md = small.tile([P, NA], F32, tag="md", name="md")
-            nc.vector.tensor_reduce(out=md[:], in_=sd[:], axis=AX.X, op=ALU.max)
             st[("sd", g)] = sd
+
+        def diag_max(g):
+            md = small.tile([P, NA], F32, tag="md", name="md")
+            nc.vector.tensor_reduce(out=md[:], in_=st[("sd", g)][:], axis=AX.X, op=ALU.max)
+            st[("md", g)] = md
+
+        def diag_bias(g):
             bd = small.tile([P, NA], F32, tag="bd", name="bd")
-            nc.vector.tensor_scalar(out=bd[:], in0=md[:], scalar1=-SCALE, scalar2=None, op0=ALU.mult)
+            nc.vector.tensor_scalar(out=bd[:], in0=st.pop(("md", g))[:], scalar1=-SCALE, scalar2=None, op0=ALU.mult)
             st[("bd", g)] = bd
             st[("bias", g)] = small.tile([P, NA], F32, tag="bias", name="bias")
             ssum = small.tile([P, NA, 2], F32, tag="ssum", name="ssum")
@@ -270,13 +272,19 @@ def tile_exactslidingwindowattention_t_kernel(tc, q, k, v, out):
                                     rhs=vc.bitcast(FP8X4), rhs_scale=vscl[:, vb, :],
                                     start=(x == 0), stop=(x == len(terms) - 1))
 
+        def row_sum(g):
+            den = small.tile([P, NA], F32, tag="den", name="den")
+            nc.vector.tensor_reduce(out=den[:], in_=st.pop(("ssum", g))[:], axis=AX.X, op=ALU.add)
+            st[("den", g)] = den
+
+        def row_recip(g):
+            rden = small.tile([P, NA], F32, tag="rden", name="rden")
+            nc.vector.reciprocal(out=rden[:], in_=st.pop(("den", g))[:])
+            st[("rden", g)] = rden
+
         def finish(g):
             b, n = g // NB, g % NB
-            ob, ssum = st.pop(("ob", g)), st.pop(("ssum", g))
-            den = small.tile([P, NA], F32, tag="den", name="den")
-            nc.vector.tensor_reduce(out=den[:], in_=ssum[:], axis=AX.X, op=ALU.add)
-            rden = small.tile([P, NA], F32, tag="rden", name="rden")
-            nc.vector.reciprocal(out=rden[:], in_=den[:])
+            ob, rden = st.pop(("ob", g)), st.pop(("rden", g))
             ost = work.tile([P, NA, D], F32, tag="ost", name="ost")
             nc.vector.tensor_tensor(out=ost[:], in0=ob[:], in1=rden[:].unsqueeze(2).to_broadcast([P, NA, D]),
                                     op=ALU.mult)
@@ -288,31 +296,36 @@ def tile_exactslidingwindowattention_t_kernel(tc, q, k, v, out):
         def okb(x):
             return 0 <= x < NBLK
 
-        for i in range(-4 * PG + LM - 1, NT + LM + 1):
-            js = i + LS
-            if ok(i - LQ):
-                quant(i - LQ)
-            if ok(js):
-                if js % NA == 0:
-                    score_diag(js // NA)
-                score(js)
-                rowmax(js)
-            if ok(i + LE):
-                expo(i + LE)
-            if ok(i):
-                transp(i)
-            if ok(i - LV):
-                evac(i - LV)
-            z = i - LM
-            if z % NA >= 2 and ok(z):
-                for a in ((0, 1) if z % NA == 2 else (2, 3)):
-                    pv(z // NA * NA + a)
-            if z % NA == NA - 1 and okb(z // NA):
-                finish(z // NA)
-            if z % NA == NA - 1 and okb(z // NA + PG):
-                prep_qk(z // NA + PG)
-                prep_v(z // NA + PG)
-            z = i - LM - 1
-            if z % NA == NA - 1 and okb(z // NA + PG):
-                copy_qk(z // NA + PG)
-                quant_v(z // NA + PG)
+        def at(s, offset, stage, *args):
+            x = s - offset
+            if x % NA == 0 and okb(x // NA):
+                stage(x // NA, *args)
+
+        def each(s, offset, stage):
+            if ok(s - offset):
+                stage(s - offset)
+
+        def pv_run(g):
+            for a in range(NA):
+                pv(g * NA + a)
+
+        with tc.manual_schedule():
+            for s in range(-8, NT + 12):
+                each(s, 2, transp)
+                at(s, -6, prep_qk)
+                each(s, -1, score)
+                at(s, 8, pv_run)
+                at(s, -3, score_diag)
+                each(s, 1, expo)
+                each(s, 3, evac)
+                each(s, 0, rowmax)
+                each(s, 4, quant)
+                at(s, -2, diag_max)
+                at(s, -1, diag_bias)
+                at(s, -1, prep_v)
+                at(s, 1, quant_v)
+                at(s, 8, row_sum)
+                at(s, 9, row_recip)
+                at(s, 10, finish)
+                at(s, -5, copy_qk, 0)
+                at(s, -4, copy_qk, 1)

@@ -26,10 +26,10 @@ NEG = -1.0e30
 FLOPS = 2 * (2 * NB - 1) * B * 2 * W * W * D
 
 CHUNKS = [1, 1, 2, 4, 4, 4, 4, 4, 4, 4]
-SM_BUFS, SD_BUFS, TP_BUFS, OB_BUFS = 2, 2, 2, 1
+SM_BUFS, SD_BUFS, TP_BUFS, OB_BUFS = 2, 2, 2, 2
 NV = 6
 NE = 2
-QK_COPY = "ad"
+QK_COPY = "aa"
 GROUPS = {1: (0, 1), 2: (2,), 3: (3, 4)}
 
 
@@ -45,7 +45,6 @@ def tile_exactslidingwindowattention_t_kernel(tc, q, k, v, out):
         ps_sd = ctx.enter_context(tc.psum_pool(name="ps_sd", bufs=SD_BUFS))
         ps_tp = ctx.enter_context(tc.psum_pool(name="ps_tp", bufs=TP_BUFS))
         ps_ob = ctx.enter_context(tc.psum_pool(name="ps_ob", bufs=OB_BUFS))
-        ps_pr = ctx.enter_context(tc.psum_pool(name="ps_pr", bufs=1))
 
         chunk_of = {}
         first = 0
@@ -112,7 +111,7 @@ def tile_exactslidingwindowattention_t_kernel(tc, q, k, v, out):
         def prep_qk(g):
             ci, jb = chunk_of[g][0], chunk_of[g][1]
             qraw, kraw = raws[ci][0], raws[ci][1]
-            tqk = ps_pr.tile([P, 2, NA, P], BF16, tag="pr", name="tqk")
+            tqk = ps_tp.tile([P, 2, NA, P], BF16, tag="tp", name="tqk")
             for a in range(NA):
                 nc.tensor.transpose(tqk[:, 0, a, :], kraw[:, jb * NA + a, :], identb[:])
             for a in range(NA):
@@ -147,13 +146,14 @@ def tile_exactslidingwindowattention_t_kernel(tc, q, k, v, out):
                 nc.sync.dma_start(out=vz[r, i:i + NA - 1, :].bitcast(I32),
                                   in_=vcodes[r, g, :].bitcast(I32).unsqueeze(1).to_broadcast([32, NA - 1, P]))
 
-        def score_diag(g):
-            sd = ps_sd.tile([P, NA, P], F32, tag="sd", name="sd")
-            for a in range(NA):
+        def score_diag(g, half):
+            if half == 0:
+                st[("sd", g)] = ps_sd.tile([P, NA, P], F32, tag="sd", name="sd")
+            sd = st[("sd", g)]
+            for a in (2 * half, 2 * half + 1):
                 c0 = g * W + a * P
                 nc.tensor.matmul(sd[:, a, :], lhsT=qt[:, c0:c0 + P], rhs=kt[:, c0:c0 + P], start=True, stop=False)
                 nc.tensor.matmul(sd[:, a, :], lhsT=identb[:], rhs=mask_d[:], start=False, stop=True)
-            st[("sd", g)] = sd
 
         def diag_max(g):
             md = small.tile([P, NA], F32, tag="md", name="md")
@@ -174,6 +174,10 @@ def tile_exactslidingwindowattention_t_kernel(tc, q, k, v, out):
             g, a = i // NA, i % NA
             return W if g % NB > 0 else a * P
 
+        def mask_oldest(i):
+            if (i // NA) % NB > 0:
+                nc.tensor.matmul(st[("sm", i)][:, 0:P], lhsT=identb[:], rhs=mask_a[:], start=False, stop=True)
+
         def score(i):
             g = i // NA
             c0 = i * P
@@ -184,7 +188,6 @@ def tile_exactslidingwindowattention_t_kernel(tc, q, k, v, out):
             st[("sm", i)] = sm
             if g % NB > 0:
                 nc.tensor.matmul(sm[:], lhsT=qt[:, c0:c0 + P], rhs=kt[:, c0 - W:c0], start=True, stop=False)
-                nc.tensor.matmul(sm[:, 0:P], lhsT=identb[:], rhs=mask_a[:], start=False, stop=True)
             else:
                 nc.tensor.matmul(sm[:, 0:nmain], lhsT=qt[:, c0:c0 + P], rhs=kt[:, g * W:g * W + nmain],
                                  start=True, stop=True)
@@ -305,27 +308,25 @@ def tile_exactslidingwindowattention_t_kernel(tc, q, k, v, out):
             if ok(s - offset):
                 stage(s - offset)
 
-        def pv_run(g):
-            for a in range(NA):
-                pv(g * NA + a)
-
         with tc.manual_schedule():
-            for s in range(-8, NT + 12):
+            for s in range(-8, NT + 13):
+                each(s, -1, score)
                 each(s, 2, transp)
                 at(s, -6, prep_qk)
-                each(s, -1, score)
-                at(s, 8, pv_run)
-                at(s, -3, score_diag)
+                each(s, -1, mask_oldest)
+                each(s, 6, pv)
+                at(s, -3, score_diag, 0)
+                at(s, -2, score_diag, 1)
                 each(s, 1, expo)
                 each(s, 3, evac)
+                at(s, 12, finish)
+                at(s, -3, prep_v)
+                at(s, -2, quant_v)
                 each(s, 0, rowmax)
+                at(s, -1, diag_max)
                 each(s, 4, quant)
-                at(s, -2, diag_max)
                 at(s, -1, diag_bias)
-                at(s, -1, prep_v)
-                at(s, 1, quant_v)
-                at(s, 8, row_sum)
-                at(s, 9, row_recip)
-                at(s, 10, finish)
+                at(s, 9, row_sum)
+                at(s, 10, row_recip)
                 at(s, -5, copy_qk, 0)
-                at(s, -4, copy_qk, 1)
+                at(s, -5, copy_qk, 1)

@@ -26,7 +26,7 @@ NEG = -1.0e30
 FLOPS = 2 * (2 * NB - 1) * B * 2 * W * W * D
 
 CHUNKS = [1, 1, 2, 4, 4, 4, 4, 4, 4, 4]
-SM_BUFS, SD_BUFS, TP_BUFS, OB_BUFS = 2, 2, 2, 2
+SM_BUFS, SD_BUFS, TP_BUFS, OB_BUFS = 3, 2, 2, 1
 NV = 6
 NE = 2
 QK_COPY = "aa"
@@ -260,20 +260,20 @@ def tile_exactslidingwindowattention_t_kernel(tc, q, k, v, out):
             for s, y in enumerate(ys):
                 st[("codes", g, y)] = (codes[:, s * P:(s + 1) * P], scl[:, s * P:(s + 1) * P])
 
-        def pv(i):
-            g, a = i // NA, i % NA
-            if a == 0:
+        def pv(g, tiles):
+            if tiles[0] == 0:
                 st[("ob", g)] = ps_ob.tile([P, NA, P], F32, tag="ob", name="ob")
             ob = st[("ob", g)]
-            terms = []
-            if g % NB > 0:
-                terms.append((a, g - 1, vcodes[:, g - 1, :] if a == 0 else vzs[(g - 1) % NV][:, 2 + a, :]))
-            terms.append((a + 1, g, vcodes[:, g, :] if a == NA - 1 else vzs[g % NV][:, a, :]))
-            for x, (y, vb, vc) in enumerate(terms):
-                codes, scl = st[("codes", g, y)]
-                nc.tensor.matmul_mx(out=ob[:, a, :], lhsT=codes.bitcast(FP8X4), lhsT_scale=scl,
-                                    rhs=vc.bitcast(FP8X4), rhs_scale=vscl[:, vb, :],
-                                    start=(x == 0), stop=(x == len(terms) - 1))
+            for a in tiles:
+                terms = []
+                if g % NB > 0:
+                    terms.append((a, g - 1, vcodes[:, g - 1, :] if a == 0 else vzs[(g - 1) % NV][:, 2 + a, :]))
+                terms.append((a + 1, g, vcodes[:, g, :] if a == NA - 1 else vzs[g % NV][:, a, :]))
+                for x, (y, vb, vc) in enumerate(terms):
+                    codes, scl = st[("codes", g, y)]
+                    nc.tensor.matmul_mx(out=ob[:, a, :], lhsT=codes.bitcast(FP8X4), lhsT_scale=scl,
+                                        rhs=vc.bitcast(FP8X4), rhs_scale=vscl[:, vb, :],
+                                        start=(x == 0), stop=(x == len(terms) - 1))
 
         def row_sum(g):
             den = small.tile([P, NA], F32, tag="den", name="den")
@@ -310,23 +310,25 @@ def tile_exactslidingwindowattention_t_kernel(tc, q, k, v, out):
 
         with tc.manual_schedule():
             for s in range(-8, NT + 13):
-                each(s, -1, score)
-                each(s, 2, transp)
-                at(s, -6, prep_qk)
-                each(s, -1, mask_oldest)
-                each(s, 6, pv)
+                each(s, -2, score)
+                at(s, 7, pv, (0, 1))
+                at(s, 8, pv, (2,))
+                at(s, 9, pv, (3,))
+                each(s, -2, mask_oldest)
                 at(s, -3, score_diag, 0)
                 at(s, -2, score_diag, 1)
+                each(s, 2, transp)
+                at(s, -6, prep_qk)
                 each(s, 1, expo)
                 each(s, 3, evac)
-                at(s, 12, finish)
-                at(s, -3, prep_v)
-                at(s, -2, quant_v)
-                each(s, 0, rowmax)
                 at(s, -1, diag_max)
-                each(s, 4, quant)
+                at(s, 10, finish)
+                each(s, 0, rowmax)
                 at(s, -1, diag_bias)
-                at(s, 9, row_sum)
-                at(s, 10, row_recip)
+                each(s, 4, quant)
+                at(s, -3, prep_v)
+                at(s, 0, quant_v)
+                at(s, 6, row_sum)
+                at(s, 8, row_recip)
                 at(s, -5, copy_qk, 0)
                 at(s, -5, copy_qk, 1)

@@ -29,7 +29,8 @@ CHUNKS = [1, 1, 2, 4, 4, 4, 4, 4, 4, 4]
 SM_BUFS, SD_BUFS, TP_BUFS, OB_BUFS = 3, 2, 2, 1
 NV = 6
 NE = 2
-QK_COPY = "aa"
+VPIECE = 32
+QK_COPY = "ad"
 GROUPS = {1: (0, 1), 2: (2,), 3: (3, 4)}
 
 
@@ -121,7 +122,7 @@ def tile_exactslidingwindowattention_t_kernel(tc, q, k, v, out):
         def copy_qk(g, s):
             dst = (kt, qt)[s]
             view = st[("tqk", g)][:, s, :, :].rearrange("p a x -> p (a x)")
-            if QK_COPY[g % 2] == "d":
+            if QK_COPY[s] == "d":
                 nc.vector.tensor_copy(out=dst[:, g * W:(g + 1) * W], in_=view)
             else:
                 nc.scalar.copy(out=dst[:, g * W:(g + 1) * W], in_=view)
@@ -130,8 +131,11 @@ def tile_exactslidingwindowattention_t_kernel(tc, q, k, v, out):
             ci, jb, nblk = chunk_of[g][0], chunk_of[g][1], chunk_of[g][2]
             vraw = raws[ci][2]
             vg = work.tile([P, D, 4], BF16, tag="vg", name="vg", align_bytes=64)
-            nc.vector.tensor_copy(out=vg[:].rearrange("p (c i) t -> p c t i", i=4),
-                                  in_=vraw[:, jb * 4:(jb + 1) * 4, :].rearrange("p t (c i) -> p c t i", i=4))
+            for d0 in range(0, D, VPIECE):
+                nc.gpsimd.tensor_scalar(
+                    out=vg[:, d0:d0 + VPIECE, :].rearrange("p (c i) t -> p c t i", i=4),
+                    in0=vraw[:, jb * 4:(jb + 1) * 4, d0:d0 + VPIECE].rearrange("p t (c i) -> p c t i", i=4),
+                    scalar1=1.0, scalar2=0.0, op0=ALU.mult, op1=ALU.add)
             st[("vg", g)] = vg
             if jb == nblk - 1 and ci + 3 < len(CHUNKS):
                 load(ci + 3)
@@ -162,7 +166,8 @@ def tile_exactslidingwindowattention_t_kernel(tc, q, k, v, out):
 
         def diag_bias(g):
             bd = small.tile([P, NA], F32, tag="bd", name="bd")
-            nc.vector.tensor_scalar(out=bd[:], in0=st.pop(("md", g))[:], scalar1=-SCALE, scalar2=None, op0=ALU.mult)
+            nc.gpsimd.tensor_scalar(out=bd[:], in0=st.pop(("md", g))[:], scalar1=-SCALE, scalar2=0.0, op0=ALU.mult,
+                                    op1=ALU.add)
             st[("bd", g)] = bd
             st[("bias", g)] = small.tile([P, NA], F32, tag="bias", name="bias")
             ssum = small.tile([P, NA, 2], F32, tag="ssum", name="ssum")
@@ -277,7 +282,8 @@ def tile_exactslidingwindowattention_t_kernel(tc, q, k, v, out):
 
         def row_sum(g):
             den = small.tile([P, NA], F32, tag="den", name="den")
-            nc.vector.tensor_reduce(out=den[:], in_=st.pop(("ssum", g))[:], axis=AX.X, op=ALU.add)
+            ssum = st.pop(("ssum", g))
+            nc.gpsimd.tensor_tensor(out=den[:], in0=ssum[:, :, 0], in1=ssum[:, :, 1], op=ALU.add)
             st[("den", g)] = den
 
         def row_recip(g):
@@ -324,11 +330,11 @@ def tile_exactslidingwindowattention_t_kernel(tc, q, k, v, out):
                 at(s, -1, diag_max)
                 at(s, 10, finish)
                 each(s, 0, rowmax)
-                at(s, -1, diag_bias)
                 each(s, 4, quant)
-                at(s, -3, prep_v)
-                at(s, 0, quant_v)
-                at(s, 6, row_sum)
+                at(s, 1, quant_v)
                 at(s, 8, row_recip)
+                at(s, -1, diag_bias)
+                at(s, -1, prep_v)
+                at(s, 6, row_sum)
                 at(s, -5, copy_qk, 0)
                 at(s, -5, copy_qk, 1)

@@ -30,7 +30,6 @@ SM_BUFS, SD_BUFS, TP_BUFS, OB_BUFS = 3, 2, 2, 1
 NV = 6
 NE = 2
 VPIECE = 32
-QK_COPY = "ad"
 GROUPS = {1: (0, 1), 2: (2,), 3: (3, 4)}
 
 
@@ -40,7 +39,7 @@ def tile_exactslidingwindowattention_t_kernel(tc, q, k, v, out):
         const = ctx.enter_context(tc.tile_pool(name="const", bufs=1))
         big = ctx.enter_context(tc.tile_pool(name="big", bufs=1))
         raw = ctx.enter_context(tc.tile_pool(name="raw", bufs=3))
-        work = ctx.enter_context(tc.tile_pool(name="work", bufs=6))
+        work = ctx.enter_context(tc.tile_pool(name="work", bufs=8))
         small = ctx.enter_context(tc.tile_pool(name="small", bufs=4))
         ps_sm = ctx.enter_context(tc.psum_pool(name="ps_sm", bufs=SM_BUFS))
         ps_sd = ctx.enter_context(tc.psum_pool(name="ps_sd", bufs=SD_BUFS))
@@ -86,6 +85,8 @@ def tile_exactslidingwindowattention_t_kernel(tc, q, k, v, out):
         nc.gpsimd.memset(maf[:], 0.0)
         nc.gpsimd.affine_select(out=maf[:], in_=maf[:], pattern=[[1, P]], compare_op=ALU.is_ge,
                                 fill=NEG, base=-1, channel_multiplier=-1)
+        minus1 = const.tile([P, NA], F32, name="minus1")
+        nc.gpsimd.memset(minus1[:], -1.0)
         mask_d = const.tile([P, P], BF16, name="mask_d")
         nc.vector.tensor_copy(out=mask_d[:], in_=mdf[:])
         mask_a = const.tile([P, P], BF16, name="mask_a")
@@ -122,7 +123,7 @@ def tile_exactslidingwindowattention_t_kernel(tc, q, k, v, out):
         def copy_qk(g, s):
             dst = (kt, qt)[s]
             view = st[("tqk", g)][:, s, :, :].rearrange("p a x -> p (a x)")
-            if QK_COPY[s] == "d":
+            if s == 1:
                 nc.vector.tensor_copy(out=dst[:, g * W:(g + 1) * W], in_=view)
             else:
                 nc.scalar.copy(out=dst[:, g * W:(g + 1) * W], in_=view)
@@ -288,7 +289,7 @@ def tile_exactslidingwindowattention_t_kernel(tc, q, k, v, out):
 
         def row_recip(g):
             rden = small.tile([P, NA], F32, tag="rden", name="rden")
-            nc.vector.reciprocal(out=rden[:], in_=st.pop(("den", g))[:])
+            nc.gpsimd.tensor_tensor(out=rden[:], in0=st.pop(("den", g))[:], in1=minus1[:], op=ALU.pow)
             st[("rden", g)] = rden
 
         def finish(g):
@@ -315,26 +316,26 @@ def tile_exactslidingwindowattention_t_kernel(tc, q, k, v, out):
                 stage(s - offset)
 
         with tc.manual_schedule():
-            for s in range(-8, NT + 13):
+            for s in range(-8, NT + 14):
+                at(s, -4, copy_qk, 1)
                 each(s, -2, score)
-                at(s, 7, pv, (0, 1))
-                at(s, 8, pv, (2,))
-                at(s, 9, pv, (3,))
+                at(s, 10, pv, (0, 1))
+                at(s, 11, pv, (2,))
+                at(s, 12, pv, (3,))
                 each(s, -2, mask_oldest)
                 at(s, -3, score_diag, 0)
-                at(s, -2, score_diag, 1)
+                at(s, -3, score_diag, 1)
                 each(s, 2, transp)
                 at(s, -6, prep_qk)
                 each(s, 1, expo)
                 each(s, 3, evac)
+                at(s, -5, copy_qk, 0)
                 at(s, -1, diag_max)
-                at(s, 10, finish)
+                at(s, 13, finish)
                 each(s, 0, rowmax)
-                each(s, 4, quant)
-                at(s, 1, quant_v)
-                at(s, 8, row_recip)
+                each(s, 5, quant)
+                at(s, 2, quant_v)
                 at(s, -1, diag_bias)
                 at(s, -1, prep_v)
                 at(s, 6, row_sum)
-                at(s, -5, copy_qk, 0)
-                at(s, -5, copy_qk, 1)
+                at(s, 6, row_recip)

@@ -92,8 +92,8 @@ def tile_exactslidingwindowattention_t_kernel(tc, q, k, v, out):
         mask_a = const.tile([P, P], BF16, name="mask_a")
         nc.vector.tensor_copy(out=mask_a[:], in_=maf[:])
 
-        qt = big.tile([P, B * S], BF16, name="qt")
-        kt = big.tile([P, B * S], BF16, name="kt")
+        qk = big.tile([P, 2, B * S], BF16, name="qk")
+        kt, qt = qk[:, 0, :], qk[:, 1, :]
         vcodes = big.tile([P, NBLK, P], U32, name="vcodes", align_bytes=64)
         vscl = big.tile([P, NBLK, P], U8, name="vscl", align_bytes=64)
         vzs = []
@@ -120,13 +120,13 @@ def tile_exactslidingwindowattention_t_kernel(tc, q, k, v, out):
                 nc.tensor.transpose(tqk[:, 1, a, :], qraw[:, jb * NA + a, :], identb[:])
             st[("tqk", g)] = tqk
 
-        def copy_qk(g, s):
-            dst = (kt, qt)[s]
-            view = st[("tqk", g)][:, s, :, :].rearrange("p a x -> p (a x)")
-            if s == 1:
-                nc.vector.tensor_copy(out=dst[:, g * W:(g + 1) * W], in_=view)
+        def copy_qk(g):
+            tqk = st.pop(("tqk", g))
+            view = tqk[:].rearrange("p s a x -> p s (a x)")
+            if g % 2 == 1:
+                nc.vector.tensor_copy(out=qk[:, :, g * W:(g + 1) * W], in_=view)
             else:
-                nc.scalar.copy(out=dst[:, g * W:(g + 1) * W], in_=view)
+                nc.scalar.copy(out=qk[:, :, g * W:(g + 1) * W], in_=view)
 
         def prep_v(g):
             ci, jb, nblk = chunk_of[g][0], chunk_of[g][1], chunk_of[g][2]
@@ -268,7 +268,10 @@ def tile_exactslidingwindowattention_t_kernel(tc, q, k, v, out):
 
         def pv(g, tiles):
             if tiles[0] == 0:
-                st[("ob", g)] = ps_ob.tile([P, NA, P], F32, tag="ob", name="ob")
+                if g == NBLK - 1:
+                    st[("ob", g)] = ps_sm.tile([P, NA, P], F32, tag="sm", name="ob_last")
+                else:
+                    st[("ob", g)] = ps_ob.tile([P, NA, P], F32, tag="ob", name="ob")
             ob = st[("ob", g)]
             for a in tiles:
                 terms = []
@@ -317,7 +320,6 @@ def tile_exactslidingwindowattention_t_kernel(tc, q, k, v, out):
 
         with tc.manual_schedule():
             for s in range(-8, NT + 14):
-                at(s, -4, copy_qk, 1)
                 each(s, -2, score)
                 at(s, 10, pv, (0, 1))
                 at(s, 11, pv, (2,))
@@ -329,13 +331,13 @@ def tile_exactslidingwindowattention_t_kernel(tc, q, k, v, out):
                 at(s, -6, prep_qk)
                 each(s, 1, expo)
                 each(s, 3, evac)
-                at(s, -5, copy_qk, 0)
-                at(s, -1, diag_max)
-                at(s, 13, finish)
                 each(s, 0, rowmax)
+                at(s, 13, finish)
+                at(s, -5, copy_qk)
                 each(s, 5, quant)
-                at(s, 2, quant_v)
-                at(s, -1, diag_bias)
-                at(s, -1, prep_v)
-                at(s, 6, row_sum)
-                at(s, 6, row_recip)
+                at(s, -2, diag_max)
+                at(s, 1, quant_v)
+                at(s, -2, diag_bias)
+                at(s, -3, prep_v)
+                at(s, 5, row_sum)
+                at(s, 5, row_recip)

@@ -36,6 +36,7 @@ GROUPS = {1: (0, 1), 2: (2,), 3: (3, 4)}
 def tile_exactslidingwindowattention_t_kernel(tc, q, k, v, out):
     nc = tc.nc
     with ExitStack() as ctx:
+        ctx.enter_context(tc.manual_schedule())
         const = ctx.enter_context(tc.tile_pool(name="const", bufs=1))
         big = ctx.enter_context(tc.tile_pool(name="big", bufs=1))
         raw = ctx.enter_context(tc.tile_pool(name="raw", bufs=3))
@@ -73,40 +74,35 @@ def tile_exactslidingwindowattention_t_kernel(tc, q, k, v, out):
         load(1)
         load(2)
 
-        identb = const.tile([P, P], BF16, name="identb")
-        masks.make_identity(nc, identb[:])
-        identf = const.tile([P, P], F32, name="identf")
-        masks.make_identity(nc, identf[:])
-        mdf = const.tile([P, P], F32, name="mdf")
-        nc.gpsimd.memset(mdf[:], 0.0)
-        nc.gpsimd.affine_select(out=mdf[:], in_=mdf[:], pattern=[[-1, P]], compare_op=ALU.is_ge,
-                                fill=NEG, base=0, channel_multiplier=1)
-        maf = const.tile([P, P], F32, name="maf")
-        nc.gpsimd.memset(maf[:], 0.0)
-        nc.gpsimd.affine_select(out=maf[:], in_=maf[:], pattern=[[1, P]], compare_op=ALU.is_ge,
-                                fill=NEG, base=-1, channel_multiplier=-1)
-        minus1 = const.tile([P, NA], F32, name="minus1")
-        nc.gpsimd.memset(minus1[:], -1.0)
-        mask_d = const.tile([P, P], BF16, name="mask_d")
-        nc.vector.tensor_copy(out=mask_d[:], in_=mdf[:])
-        mask_a = const.tile([P, P], BF16, name="mask_a")
-        nc.vector.tensor_copy(out=mask_a[:], in_=maf[:])
-
         qk = big.tile([P, 2, B * S], BF16, name="qk")
         kt, qt = qk[:, 0, :], qk[:, 1, :]
         vcodes = big.tile([P, NBLK, P], U32, name="vcodes", align_bytes=64)
         vscl = big.tile([P, NBLK, P], U8, name="vscl", align_bytes=64)
-        vzs = []
-        for s in range(NV):
-            vz = big.tile([P, 2 * (NA - 1), P], U32, name="vz%d" % s, align_bytes=64)
-            nc.gpsimd.memset(vz[:], 0)
+        vzs, ebs = [], []
+        for n in range(NV):
+            vz = big.tile([P, 2 * (NA - 1), P], U32, name="vz%d" % n, align_bytes=64)
             vzs.append(vz)
-        ebs = []
-        for s in range(NE):
-            eb = big.tile([P, 2, 2 * RW], BF16, name="eb%d" % s)
-            if s == 0:
-                nc.vector.memset(eb[:], 0.0)
+        for n in range(NE):
+            eb = big.tile([P, 2, 2 * RW], BF16, name="eb%d" % n)
             ebs.append(eb)
+        nc.vector.memset(ebs[0][:].bitcast(U32), 0)
+        for n in range(NV):
+            nc.vector.memset(vzs[n][:], 0)
+
+        identb = const.tile([P, P], BF16, name="identb")
+        masks.make_identity(nc, identb[:])
+        mask_d = const.tile([P, P], BF16, name="mask_d")
+        nc.gpsimd.memset(mask_d[:], 0.0)
+        nc.gpsimd.affine_select(out=mask_d[:], in_=mask_d[:], pattern=[[-1, P]], compare_op=ALU.is_ge,
+                                fill=NEG, base=0, channel_multiplier=1)
+        mask_a = const.tile([P, P], BF16, name="mask_a")
+        nc.gpsimd.memset(mask_a[:], 0.0)
+        nc.gpsimd.affine_select(out=mask_a[:], in_=mask_a[:], pattern=[[1, P]], compare_op=ALU.is_ge,
+                                fill=NEG, base=-1, channel_multiplier=-1)
+        identf = const.tile([P, P], F32, name="identf")
+        masks.make_identity(nc, identf[:])
+        minus1 = const.tile([P, NA], F32, name="minus1")
+        nc.gpsimd.memset(minus1[:], -1.0)
 
         st = {}
 
@@ -119,6 +115,8 @@ def tile_exactslidingwindowattention_t_kernel(tc, q, k, v, out):
             for a in range(NA):
                 nc.tensor.transpose(tqk[:, 1, a, :], qraw[:, jb * NA + a, :], identb[:])
             st[("tqk", g)] = tqk
+            if jb == chunk_of[g][2] - 1 and ci + 3 < len(CHUNKS):
+                load(ci + 3)
 
         def copy_qk(g):
             tqk = st.pop(("tqk", g))
@@ -138,8 +136,6 @@ def tile_exactslidingwindowattention_t_kernel(tc, q, k, v, out):
                     in0=vraw[:, jb * 4:(jb + 1) * 4, d0:d0 + VPIECE].rearrange("p t (c i) -> p c t i", i=4),
                     scalar1=1.0, scalar2=0.0, op0=ALU.mult, op1=ALU.add)
             st[("vg", g)] = vg
-            if jb == nblk - 1 and ci + 3 < len(CHUNKS):
-                load(ci + 3)
 
         def quant_v(g):
             vg = st.pop(("vg", g))
@@ -151,14 +147,13 @@ def tile_exactslidingwindowattention_t_kernel(tc, q, k, v, out):
                 nc.sync.dma_start(out=vz[r, i:i + NA - 1, :].bitcast(I32),
                                   in_=vcodes[r, g, :].bitcast(I32).unsqueeze(1).to_broadcast([32, NA - 1, P]))
 
-        def score_diag(g, half):
-            if half == 0:
-                st[("sd", g)] = ps_sd.tile([P, NA, P], F32, tag="sd", name="sd")
-            sd = st[("sd", g)]
-            for a in (2 * half, 2 * half + 1):
+        def score_diag(g):
+            sd = ps_sd.tile([P, NA, P], F32, tag="sd", name="sd")
+            for a in range(NA):
                 c0 = g * W + a * P
                 nc.tensor.matmul(sd[:, a, :], lhsT=qt[:, c0:c0 + P], rhs=kt[:, c0:c0 + P], start=True, stop=False)
                 nc.tensor.matmul(sd[:, a, :], lhsT=identb[:], rhs=mask_d[:], start=False, stop=True)
+            st[("sd", g)] = sd
 
         def diag_max(g):
             md = small.tile([P, NA], F32, tag="md", name="md")
@@ -166,15 +161,15 @@ def tile_exactslidingwindowattention_t_kernel(tc, q, k, v, out):
             st[("md", g)] = md
 
         def diag_bias(g):
+            ssum = small.tile([P, NA, 2], F32, tag="ssum", name="ssum")
+            if g % NB == 0:
+                nc.gpsimd.memset(ssum[:], 0.0)
+            st[("ssum", g)] = ssum
             bd = small.tile([P, NA], F32, tag="bd", name="bd")
             nc.gpsimd.tensor_scalar(out=bd[:], in0=st.pop(("md", g))[:], scalar1=-SCALE, scalar2=0.0, op0=ALU.mult,
                                     op1=ALU.add)
             st[("bd", g)] = bd
             st[("bias", g)] = small.tile([P, NA], F32, tag="bias", name="bias")
-            ssum = small.tile([P, NA, 2], F32, tag="ssum", name="ssum")
-            if g % NB == 0:
-                nc.vector.memset(ssum[:], 0.0)
-            st[("ssum", g)] = ssum
 
         def n_main(i):
             g, a = i // NA, i % NA
@@ -204,9 +199,10 @@ def tile_exactslidingwindowattention_t_kernel(tc, q, k, v, out):
             if nmain == 0:
                 return
             sm = st.pop(("sm", i))
-            ss = work.tile([P, W], F32, tag="ss", name="ss")
+            ss = work.tile([P, 2, W // 2], F32, tag="ss", name="ss")
             st[("ss", i)] = ss
-            nc.vector.tensor_scalar(out=ss[:, 0:nmain], in0=sm[:, 0:nmain], scalar1=-SCALE,
+            nc.vector.tensor_scalar(out=ss[:, :, 0:nmain // 2].rearrange("p u (x e) -> p u x e", e=2),
+                                    in0=sm[:, 0:nmain].rearrange("p (x u e) -> p u x e", u=2, e=2), scalar1=-SCALE,
                                     scalar2=st[("bd", g)][:, a:a + 1], op0=ALU.mult, op1=ALU.min,
                                     accum_out=st[("bias", g)][:, a:a + 1])
 
@@ -221,7 +217,7 @@ def tile_exactslidingwindowattention_t_kernel(tc, q, k, v, out):
             if nmain > 0:
                 ss = st.pop(("ss", i))
                 nc.scalar.activation(out=eb[:, :, dg - nmain // 2:dg].rearrange("p u (x e) -> p u x e", e=2),
-                                     in_=ss[:, 0:nmain].rearrange("p (x u e) -> p u x e", u=2, e=2),
+                                     in_=ss[:, :, 0:nmain // 2].rearrange("p u (x e) -> p u x e", e=2),
                                      func=ACTF.Exp, bias=bias[:, a:a + 1], scale=-1.0, accum_out=ssum[:, a, 0:1])
             nc.scalar.activation(out=eb[:, :, dg:end].rearrange("p u (x e) -> p u x e", e=2),
                                  in_=sd[:, a, :].rearrange("p (x u e) -> p u x e", u=2, e=2),
@@ -318,26 +314,24 @@ def tile_exactslidingwindowattention_t_kernel(tc, q, k, v, out):
             if ok(s - offset):
                 stage(s - offset)
 
-        with tc.manual_schedule():
-            for s in range(-8, NT + 14):
-                each(s, -2, score)
-                at(s, 10, pv, (0, 1))
-                at(s, 11, pv, (2,))
-                at(s, 12, pv, (3,))
-                each(s, -2, mask_oldest)
-                at(s, -3, score_diag, 0)
-                at(s, -3, score_diag, 1)
-                each(s, 2, transp)
-                at(s, -6, prep_qk)
-                each(s, 1, expo)
-                each(s, 3, evac)
-                each(s, 0, rowmax)
-                at(s, 13, finish)
-                at(s, -5, copy_qk)
-                each(s, 5, quant)
-                at(s, -2, diag_max)
-                at(s, 1, quant_v)
-                at(s, -2, diag_bias)
-                at(s, -3, prep_v)
-                at(s, 5, row_sum)
-                at(s, 5, row_recip)
+        for s in range(-8, NT + 14):
+            each(s, -2, score)
+            at(s, 10, pv, (0, 1))
+            at(s, 11, pv, (2,))
+            at(s, 12, pv, (3,))
+            each(s, -2, mask_oldest)
+            at(s, -3, score_diag)
+            each(s, 2, transp)
+            at(s, -6, prep_qk)
+            each(s, 1, expo)
+            each(s, 3, evac)
+            each(s, 0, rowmax)
+            at(s, 13, finish)
+            at(s, -5, copy_qk)
+            each(s, 5, quant)
+            at(s, -2, diag_max)
+            at(s, -3, quant_v)
+            at(s, -2, diag_bias)
+            at(s, -7, prep_v)
+            at(s, 5, row_sum)
+            at(s, 5, row_recip)

from contextlib import ExitStack

import concourse.masks as masks
import concourse.mybir as mybir

F32 = mybir.dt.float32
BF16 = mybir.dt.bfloat16
U32 = mybir.dt.uint32
I32 = mybir.dt.int32
U8 = mybir.dt.uint8
FP8X4 = mybir.dt.float8_e4m3fn_x4
ACTF = mybir.ActivationFunctionType
ALU = mybir.AluOpType
AX = mybir.AxisListType

B, S, D, W = 2, 8192, 128, 512
P = 128
NB = S // W
NA = W // P
NBLK = B * NB
NT = NBLK * NA
NY = NA + 1
RW = NY * P
SCALE = D ** -0.5
NEG = -1.0e30
FLOPS = 2 * (2 * NB - 1) * B * 2 * W * W * D

CHUNKS = [1, 1, 2, 4, 4, 4, 4, 4, 4, 4]
SM_BUFS, SD_BUFS, TP_BUFS, OB_BUFS = 3, 2, 2, 1
NV = 6
NE = 2
VPIECE = 32
GROUPS = {1: (0, 1), 2: (2,), 3: (3, 4)}


def tile_exactslidingwindowattention_t_kernel(tc, q, k, v, out):
    nc = tc.nc
    with ExitStack() as ctx:
        ctx.enter_context(tc.manual_schedule())
        const = ctx.enter_context(tc.tile_pool(name="const", bufs=1))
        big = ctx.enter_context(tc.tile_pool(name="big", bufs=1))
        raw = ctx.enter_context(tc.tile_pool(name="raw", bufs=3))
        work = ctx.enter_context(tc.tile_pool(name="work", bufs=8))
        small = ctx.enter_context(tc.tile_pool(name="small", bufs=4))
        ps_sm = ctx.enter_context(tc.psum_pool(name="ps_sm", bufs=SM_BUFS))
        ps_sd = ctx.enter_context(tc.psum_pool(name="ps_sd", bufs=SD_BUFS))
        ps_tp = ctx.enter_context(tc.psum_pool(name="ps_tp", bufs=TP_BUFS))
        ps_ob = ctx.enter_context(tc.psum_pool(name="ps_ob", bufs=OB_BUFS))

        chunk_of = {}
        first = 0
        for ci, nblk in enumerate(CHUNKS):
            for jb in range(nblk):
                chunk_of[first + jb] = (ci, jb, nblk, first)
            first += nblk
        raws = {}

        def load(ci):
            nblk = CHUNKS[ci]
            g0 = sum(CHUNKS[:ci])
            b, r0, rows = g0 // NB, (g0 % NB) * W, nblk * W
            kraw = raw.tile([P, 4 * NA, D], BF16, tag="kraw", name="kraw")
            nc.sync.dma_start(out=kraw[:, 0:nblk * NA, :],
                              in_=k[b, r0:r0 + rows, :].rearrange("(j p) d -> p j d", p=P))
            qraw = raw.tile([P, 4 * NA, D], BF16, tag="qraw", name="qraw")
            nc.sync.dma_start(out=qraw[:, 0:nblk * NA, :],
                              in_=q[b, r0:r0 + rows, :].rearrange("(j p) d -> p j d", p=P))
            vraw = raw.tile([P, 4 * 4, D], BF16, tag="vraw", name="vraw")
            nc.sync.dma_start(out=vraw[:, 0:nblk * 4, :].rearrange("p (m t) d -> p m (t d)", t=4),
                              in_=v[b, r0:r0 + rows, :].rearrange("(m p t) d -> p m (t d)", p=P, t=4))
            raws[ci] = (qraw, kraw, vraw)

        load(0)
        load(1)
        load(2)

        qk = big.tile([P, 2, B * S], BF16, name="qk")
        kt, qt = qk[:, 0, :], qk[:, 1, :]
        vcodes = big.tile([P, NBLK, P], U32, name="vcodes", align_bytes=64)
        vscl = big.tile([P, NBLK, P], U8, name="vscl", align_bytes=64)
        vzs, ebs = [], []
        for n in range(NV):
            vz = big.tile([P, 2 * (NA - 1), P], U32, name="vz%d" % n, align_bytes=64)
            vzs.append(vz)
        for n in range(NE):
            eb = big.tile([P, 2, 2 * RW], BF16, name="eb%d" % n)
            ebs.append(eb)
        nc.vector.memset(ebs[0][:].bitcast(U32), 0)
        for n in range(NV):
            nc.vector.memset(vzs[n][:], 0)

        identb = const.tile([P, P], BF16, name="identb")
        masks.make_identity(nc, identb[:])
        mask_d = const.tile([P, P], BF16, name="mask_d")
        nc.gpsimd.memset(mask_d[:], 0.0)
        nc.gpsimd.affine_select(out=mask_d[:], in_=mask_d[:], pattern=[[-1, P]], compare_op=ALU.is_ge,
                                fill=NEG, base=0, channel_multiplier=1)
        mask_a = const.tile([P, P], BF16, name="mask_a")
        nc.gpsimd.memset(mask_a[:], 0.0)
        nc.gpsimd.affine_select(out=mask_a[:], in_=mask_a[:], pattern=[[1, P]], compare_op=ALU.is_ge,
                                fill=NEG, base=-1, channel_multiplier=-1)
        identf = const.tile([P, P], F32, name="identf")
        masks.make_identity(nc, identf[:])
        minus1 = const.tile([P, NA], F32, name="minus1")
        nc.gpsimd.memset(minus1[:], -1.0)

        st = {}

        def prep_qk(g):
            ci, jb = chunk_of[g][0], chunk_of[g][1]
            qraw, kraw = raws[ci][0], raws[ci][1]
            tqk = ps_tp.tile([P, 2, NA, P], BF16, tag="tp", name="tqk")
            for a in range(NA):
                nc.tensor.transpose(tqk[:, 0, a, :], kraw[:, jb * NA + a, :], identb[:])
            for a in range(NA):
                nc.tensor.transpose(tqk[:, 1, a, :], qraw[:, jb * NA + a, :], identb[:])
            st[("tqk", g)] = tqk
            if jb == chunk_of[g][2] - 1 and ci + 3 < len(CHUNKS):
                load(ci + 3)

        def copy_qk(g):
            tqk = st.pop(("tqk", g))
            view = tqk[:].rearrange("p s a x -> p s (a x)")
            if g % 2 == 1:
                nc.vector.tensor_copy(out=qk[:, :, g * W:(g + 1) * W], in_=view)
            else:
                nc.scalar.copy(out=qk[:, :, g * W:(g + 1) * W], in_=view)

        def prep_v(g):
            ci, jb, nblk = chunk_of[g][0], chunk_of[g][1], chunk_of[g][2]
            vraw = raws[ci][2]
            vg = work.tile([P, D, 4], BF16, tag="vg", name="vg", align_bytes=64)
            for d0 in range(0, D, VPIECE):
                nc.gpsimd.tensor_scalar(
                    out=vg[:, d0:d0 + VPIECE, :].rearrange("p (c i) t -> p c t i", i=4),
                    in0=vraw[:, jb * 4:(jb + 1) * 4, d0:d0 + VPIECE].rearrange("p t (c i) -> p c t i", i=4),
                    scalar1=1.0, scalar2=0.0, op0=ALU.mult, op1=ALU.add)
            st[("vg", g)] = vg

        def quant_v(g):
            vg = st.pop(("vg", g))
            nc.vector.quantize_mx(out=vcodes[:, g, :].bitcast(FP8X4), scales=vscl[:, g, :],
                                  in_=vg[:].rearrange("p d t -> p (d t)"))
            vz = vzs[g % NV]
            for i in range(NA):
                r = slice(i * 32, (i + 1) * 32)
                nc.sync.dma_start(out=vz[r, i:i + NA - 1, :].bitcast(I32),
                                  in_=vcodes[r, g, :].bitcast(I32).unsqueeze(1).to_broadcast([32, NA - 1, P]))

        def score_diag(g):
            sd = ps_sd.tile([P, NA, P], F32, tag="sd", name="sd")
            for a in range(NA):
                c0 = g * W + a * P
                nc.tensor.matmul(sd[:, a, :], lhsT=qt[:, c0:c0 + P], rhs=kt[:, c0:c0 + P], start=True, stop=False)
                nc.tensor.matmul(sd[:, a, :], lhsT=identb[:], rhs=mask_d[:], start=False, stop=True)
            st[("sd", g)] = sd

        def diag_max(g):
            md = small.tile([P, NA], F32, tag="md", name="md")
            nc.vector.tensor_reduce(out=md[:], in_=st[("sd", g)][:], axis=AX.X, op=ALU.max)
            st[("md", g)] = md

        def diag_bias(g):
            ssum = small.tile([P, NA, 2], F32, tag="ssum", name="ssum")
            if g % NB == 0:
                nc.gpsimd.memset(ssum[:], 0.0)
            st[("ssum", g)] = ssum
            bd = small.tile([P, NA], F32, tag="bd", name="bd")
            nc.gpsimd.tensor_scalar(out=bd[:], in0=st.pop(("md", g))[:], scalar1=-SCALE, scalar2=0.0, op0=ALU.mult,
                                    op1=ALU.add)
            st[("bd", g)] = bd
            st[("bias", g)] = small.tile([P, NA], F32, tag="bias", name="bias")

        def n_main(i):
            g, a = i // NA, i % NA
            return W if g % NB > 0 else a * P

        def mask_oldest(i):
            if (i // NA) % NB > 0:
                nc.tensor.matmul(st[("sm", i)][:, 0:P], lhsT=identb[:], rhs=mask_a[:], start=False, stop=True)

        def score(i):
            g = i // NA
            c0 = i * P
            nmain = n_main(i)
            if nmain == 0:
                return
            sm = ps_sm.tile([P, W], F32, tag="sm", name="sm")
            st[("sm", i)] = sm
            if g % NB > 0:
                nc.tensor.matmul(sm[:], lhsT=qt[:, c0:c0 + P], rhs=kt[:, c0 - W:c0], start=True, stop=False)
            else:
                nc.tensor.matmul(sm[:, 0:nmain], lhsT=qt[:, c0:c0 + P], rhs=kt[:, g * W:g * W + nmain],
                                 start=True, stop=True)

        def rowmax(i):
            g, a = i // NA, i % NA
            nmain = n_main(i)
            if nmain == 0:
                return
            sm = st.pop(("sm", i))
            ss = work.tile([P, 2, W // 2], F32, tag="ss", name="ss")
            st[("ss", i)] = ss
            nc.vector.tensor_scalar(out=ss[:, :, 0:nmain // 2].rearrange("p u (x e) -> p u x e", e=2),
                                    in0=sm[:, 0:nmain].rearrange("p (x u e) -> p u x e", u=2, e=2), scalar1=-SCALE,
                                    scalar2=st[("bd", g)][:, a:a + 1], op0=ALU.mult, op1=ALU.min,
                                    accum_out=st[("bias", g)][:, a:a + 1])

        def expo(i):
            g, a = i // NA, i % NA
            nmain = n_main(i)
            eb = ebs[g % NE]
            ssum, sd = st[("ssum", g)], st[("sd", g)]
            bias = st[("bias", g)] if nmain > 0 else st[("bd", g)]
            end = (a + 1) * 2 * (P + 32)
            dg = end - P // 2
            if nmain > 0:
                ss = st.pop(("ss", i))
                nc.scalar.activation(out=eb[:, :, dg - nmain // 2:dg].rearrange("p u (x e) -> p u x e", e=2),
                                     in_=ss[:, :, 0:nmain // 2].rearrange("p u (x e) -> p u x e", e=2),
                                     func=ACTF.Exp, bias=bias[:, a:a + 1], scale=-1.0, accum_out=ssum[:, a, 0:1])
            nc.scalar.activation(out=eb[:, :, dg:end].rearrange("p u (x e) -> p u x e", e=2),
                                 in_=sd[:, a, :].rearrange("p (x u e) -> p u x e", u=2, e=2),
                                 func=ACTF.Exp, bias=bias[:, a:a + 1], scale=SCALE, accum_out=ssum[:, a, 1:2])

        def groups(i):
            g, a = i // NA, i % NA
            ys = GROUPS.get(a, ())
            return [y for y in ys if y > 0 or g % NB > 0]

        def transp(i):
            ys = groups(i)
            if not ys:
                return
            ew = ebs[(i // NA) % NE][:].bitcast(F32)
            tp = ps_tp.tile([P, len(ys), 2, P], F32, tag="tp", name="tp")
            for s, y in enumerate(ys):
                for u in range(2):
                    nc.tensor.transpose(tp[:, s, u, :], ew[:, u, y * P:(y + 1) * P], identf[:])
            st[("tp", i)] = tp

        def evac(i):
            n = len(groups(i))
            if n == 0:
                return
            tp = st.pop(("tp", i))
            gr = work.tile([P, n, P, 2], F32, tag="gr", name="gr", align_bytes=64)
            nc.scalar.copy(out=gr[:], in_=tp[:].rearrange("p s u r -> p s r u"))
            st[("gr", i)] = gr

        def quant(i):
            g = i // NA
            ys = groups(i)
            if not ys:
                return
            n = len(ys)
            gr = st.pop(("gr", i))
            codes = work.tile([P, n * P], U32, tag="codes", name="codes", align_bytes=64)
            scl = work.tile([P, n * P], U8, tag="scl", name="scl", align_bytes=64)
            nc.vector.quantize_mx(out=codes[:].bitcast(FP8X4), scales=scl[:],
                                  in_=gr[:].rearrange("p s r u -> p (s r u)").bitcast(BF16))
            for s, y in enumerate(ys):
                st[("codes", g, y)] = (codes[:, s * P:(s + 1) * P], scl[:, s * P:(s + 1) * P])

        def pv(g, tiles):
            if tiles[0] == 0:
                if g == NBLK - 1:
                    st[("ob", g)] = ps_sm.tile([P, NA, P], F32, tag="sm", name="ob_last")
                else:
                    st[("ob", g)] = ps_ob.tile([P, NA, P], F32, tag="ob", name="ob")
            ob = st[("ob", g)]
            for a in tiles:
                terms = []
                if g % NB > 0:
                    terms.append((a, g - 1, vcodes[:, g - 1, :] if a == 0 else vzs[(g - 1) % NV][:, 2 + a, :]))
                terms.append((a + 1, g, vcodes[:, g, :] if a == NA - 1 else vzs[g % NV][:, a, :]))
                for x, (y, vb, vc) in enumerate(terms):
                    codes, scl = st[("codes", g, y)]
                    nc.tensor.matmul_mx(out=ob[:, a, :], lhsT=codes.bitcast(FP8X4), lhsT_scale=scl,
                                        rhs=vc.bitcast(FP8X4), rhs_scale=vscl[:, vb, :],
                                        start=(x == 0), stop=(x == len(terms) - 1))

        def row_sum(g):
            den = small.tile([P, NA], F32, tag="den", name="den")
            ssum = st.pop(("ssum", g))
            nc.gpsimd.tensor_tensor(out=den[:], in0=ssum[:, :, 0], in1=ssum[:, :, 1], op=ALU.add)
            st[("den", g)] = den

        def row_recip(g):
            rden = small.tile([P, NA], F32, tag="rden", name="rden")
            nc.gpsimd.tensor_tensor(out=rden[:], in0=st.pop(("den", g))[:], in1=minus1[:], op=ALU.pow)
            st[("rden", g)] = rden

        def finish(g):
            b, n = g // NB, g % NB
            ob, rden = st.pop(("ob", g)), st.pop(("rden", g))
            ost = work.tile([P, NA, D], F32, tag="ost", name="ost")
            nc.vector.tensor_tensor(out=ost[:], in0=ob[:], in1=rden[:].unsqueeze(2).to_broadcast([P, NA, D]),
                                    op=ALU.mult)
            nc.sync.dma_start(out=out[b, n * W:(n + 1) * W, :].rearrange("(a p) d -> p a d", p=P), in_=ost[:])

        def ok(x):
            return 0 <= x < NT

        def okb(x):
            return 0 <= x < NBLK

        def at(s, offset, stage, *args):
            x = s - offset
            if x % NA == 0 and okb(x // NA):
                stage(x // NA, *args)

        def each(s, offset, stage):
            if ok(s - offset):
                stage(s - offset)

        for s in range(-8, NT + 14):
            each(s, -2, score)
            at(s, 10, pv, (0, 1))
            at(s, 11, pv, (2,))
            at(s, 12, pv, (3,))
            each(s, -2, mask_oldest)
            at(s, -3, score_diag)
            each(s, 2, transp)
            at(s, -6, prep_qk)
            each(s, 1, expo)
            each(s, 3, evac)
            each(s, 0, rowmax)
            at(s, 13, finish)
            at(s, -5, copy_qk)
            each(s, 5, quant)
            at(s, -2, diag_max)
            at(s, -3, quant_v)
            at(s, -2, diag_bias)
            at(s, -7, prep_v)
            at(s, 5, row_sum)
            at(s, 5, row_recip)
